import numpy as np
import ml_dtypes


def mxq(x, axis, fmt="e4m3"):
    dtype, down = {"e4m3": (ml_dtypes.float8_e4m3fn, 7), "e5m2": (ml_dtypes.float8_e5m2, 14)}[fmt]
    v = np.moveaxis(np.asarray(x, np.float32).astype(ml_dtypes.bfloat16).astype(np.float64), axis, -1)
    blocks = v.reshape(v.shape[:-1] + (-1, 32))
    amax = np.abs(blocks).max(-1, keepdims=True)
    byte = np.maximum(np.where(amax > 0, np.frexp(amax)[1] - 1 + 127, 0) - down, 1)
    scale = np.exp2(byte - 127.0)
    codes = (blocks / scale).astype(np.float32).astype(dtype).astype(np.float64)
    return np.moveaxis((codes * scale).reshape(v.shape), -1, axis)


WIDE = False


def mx_kscale(k):
    if not WIDE:
        return np.ones(k)
    levels = np.array([10, -10, 5, -5, 0])
    a = np.random.permutation(np.resize(levels, k // 512 * 4)).reshape(k // 512, 4)
    idx = np.arange(k)
    return np.exp2(a[idx // 512, idx % 128 // 32])


BF16 = ml_dtypes.bfloat16


def bf(x):
    return np.asarray(x, np.float32).astype(BF16)


def f64(x):
    return np.asarray(x).astype(np.float64)


E2M1 = np.array([0.0, 0.5, 1.0, 1.5, 2.0, 3.0, 4.0, 6.0, -0.0, -0.5, -1.0, -1.5, -2.0, -3.0, -4.0, -6.0])


def pack_weight(w, fmt):
    k, n = w.shape
    w = f64(bf(w)).reshape(k // 32, 32, n)
    amax = np.abs(w).max(1)
    if fmt == "e4m3":
        byte = np.frexp(amax)[1] - 1 + 127 - 7
    else:
        mant, ex = np.frexp(amax / 6.0)
        byte = np.where(mant > 0.5, ex, ex - 1) + 127
    byte = np.clip(np.where(amax > 0, byte, 1), 1, 254)
    scaled = (w * np.exp2(127.0 - byte)[:, None, :]).reshape(k, n).astype(np.float32)
    by_word = np.ascontiguousarray(scaled.reshape(k // 512, 128, 4, n).transpose(0, 1, 3, 2))
    if fmt == "e4m3":
        words = by_word.astype(ml_dtypes.float8_e4m3fn).view(np.uint8)
    else:
        c = by_word.astype(ml_dtypes.float4_e2m1fn).view(np.uint8) & 0xF
        words = c[..., 0::2] | (c[..., 1::2] << 4)
    return np.ascontiguousarray(words), np.ascontiguousarray(byte.astype(np.uint8).reshape(k // 512, 16, n))


def unpack_weight(words, scales, fmt):
    g, p, n, _ = words.shape
    if fmt == "e4m3":
        vals = np.ascontiguousarray(words).view(ml_dtypes.float8_e4m3fn).astype(np.float64)
    else:
        nib = np.empty((g, p, n, 4), np.uint8)
        nib[..., 0::2] = words & 0xF
        nib[..., 1::2] = words >> 4
        vals = E2M1[nib]
    vals = vals * np.repeat(np.exp2(scales.astype(np.float64) - 127.0), 8, axis=1)[..., None]
    return vals.transpose(0, 1, 3, 2).reshape(g * 512, n)


B, N, D = 4, 512, 512
C = 2 * D
EPS_L1 = 1e-12
EPS_BN = 1e-5
NEG_SLOPE = 0.01
FMT = "e4m3"


def l1_normalize(x):
    return x / np.maximum(np.sum(np.abs(x), axis=-1, keepdims=True), EPS_L1)


def bn_lrelu(x, g, b):
    mean = np.mean(x, axis=(0, 2), keepdims=True)
    var = np.var(x, axis=(0, 2), keepdims=True)
    y = (x - mean) / np.sqrt(var + EPS_BN) * g[None, :, None] + b[None, :, None]
    return np.where(y >= 0, y, NEG_SLOPE * y)


def draw_edge():
    u = 1.5 * np.random.random_sample((B, N, N)) - 0.5 + 2.0 * np.eye(N)
    return bf(u * np.exp(0.5 * np.random.standard_normal((B, N, 1))))


def setup_inputs():
    t = mx_kscale(C)[:D]
    tt = np.concatenate([t, t])
    distribution_edge = draw_edge()
    instance_edge = draw_edge()
    point_node = bf(np.random.standard_normal((B, N, D)) * 0.2 * np.sqrt(N) * t)
    w1 = np.random.standard_normal((C, C)) * 2.0 / np.sqrt(C) / tt[None, :]
    W1_words, W1_scales = pack_weight(np.ascontiguousarray(w1.T), FMT)
    g1 = bf(1.0 + 0.2 * np.random.standard_normal(C))
    b1 = bf(0.3 * np.random.standard_normal(C))
    return {"distribution_edge": distribution_edge,
            "instance_edge": instance_edge,
            "point_node": point_node,
            "W1_words": W1_words,
            "W1_scales": W1_scales,
            "g1": g1,
            "b1": b1}


def reference(distribution_edge, instance_edge, point_node, W1_words, W1_scales, g1, b1):
    diag_mask = 1.0 - np.eye(N)
    pq = mxq(f64(point_node), 1, "e4m3")
    edge_feat = l1_normalize(f64(distribution_edge) * diag_mask)
    aggr_feat = mxq(edge_feat, 2, "e4m3") @ pq
    edge_instance = l1_normalize(f64(instance_edge) * diag_mask)
    aggr_instance = mxq(edge_instance, 2, "e4m3") @ pq
    x = np.concatenate([aggr_feat, aggr_instance], axis=-1)
    x = np.swapaxes(x, 1, 2)
    w = unpack_weight(W1_words, W1_scales, FMT)
    z = w.T @ mxq(x, 1, "e4m3")
    return bn_lrelu(z, f64(g1), f64(b1))

@@ -1,0 +1,227 @@
+from contextlib import ExitStack
+
+import concourse.mybir as mybir
+from concourse.masks import make_identity
+
+F32 = mybir.dt.float32
+BF16 = mybir.dt.bfloat16
+I32 = mybir.dt.int32
+U32 = mybir.dt.uint32
+U8 = mybir.dt.uint8
+FP8X4 = mybir.dt.float8_e4m3fn_x4
+ALU = mybir.AluOpType
+ACT = mybir.ActivationFunctionType
+
+P = 128
+PACK = 4
+GRAPHS = 4
+NODES = 512
+FEATURES = 512
+CHANNELS = 2 * FEATURES
+NODE_TILES = NODES // P
+CHANNEL_TILES = CHANNELS // P
+K_GROUPS = CHANNELS // (P * PACK)
+EPS_L1 = 1e-12
+EPS_BN = 1e-5
+NEG_SLOPE = 0.01
+BN_STATS_DIM = 6
+
+FLOPS = 2 * GRAPHS * (2 * NODES * NODES * FEATURES + CHANNELS * CHANNELS * NODES)
+
+
+def tile_yuyipointupdate_pa_kernel(
+    tc, distribution_edge, instance_edge, point_node, W1_words, W1_scales, g1, b1, out
+):
+    nc = tc.nc
+    edges = (distribution_edge, instance_edge)
+
+    with ExitStack() as ctx:
+        const = ctx.enter_context(tc.tile_pool(name="const", bufs=1))
+        inputs = ctx.enter_context(tc.tile_pool(name="inputs", bufs=1))
+        keep = ctx.enter_context(tc.tile_pool(name="keep", bufs=1))
+        work = ctx.enter_context(tc.tile_pool(name="work", bufs=3))
+        small = ctx.enter_context(tc.tile_pool(name="small", bufs=4))
+
+        ident_f32 = const.tile([P, P], F32)
+        make_identity(nc, ident_f32[:])
+        ident_bf16 = const.tile([P, P], BF16)
+        make_identity(nc, ident_bf16[:])
+        off_diagonal = const.tile([P, P], BF16)
+        nc.vector.tensor_scalar(
+            out=off_diagonal[:], in0=ident_bf16[:], scalar1=-1.0, scalar2=1.0, op0=ALU.mult, op1=ALU.add
+        )
+        eps_bn = const.tile([P, 1], F32)
+        nc.vector.memset(eps_bn[:], EPS_BN)
+        gain_shift_rows = const.tile([P, P], BF16)
+        nc.vector.memset(gain_shift_rows[:], 0.0)
+        w_scales = keep.tile([P, K_GROUPS, CHANNELS], U8, align_bytes=64)
+        nc.vector.memset(w_scales[:].rearrange("p g n -> p (g n)").bitcast(I32), 0)
+
+        edge_sb = {}
+        point_raw = {}
+        for b in range(GRAPHS):
+            for e in range(2):
+                edge_sb[b, e] = inputs.tile([P, NODE_TILES, NODES], BF16, name="edge_%d_%d" % (b, e))
+                nc.sync.dma_start(out=edge_sb[b, e][:], in_=edges[e][b].rearrange("(r p) m -> p r m", p=P))
+            point_raw[b] = inputs.tile([P, PACK, FEATURES], BF16, name="point_%d" % b)
+            nc.sync.dma_start(
+                out=point_raw[b][:].rearrange("q (u e) d -> q u e d", u=2),
+                in_=point_node[b].rearrange("(u q e) d -> q u e d", u=2, e=2),
+            )
+        nc.sync.dma_start(out=gain_shift_rows[0:CHANNEL_TILES, :], in_=g1.rearrange("(t p) -> t p", p=P))
+        nc.sync.dma_start(
+            out=gain_shift_rows[CHANNEL_TILES : 2 * CHANNEL_TILES, :], in_=b1.rearrange("(t p) -> t p", p=P)
+        )
+        w_words = keep.tile([P, K_GROUPS, CHANNELS], U32, align_bytes=64)
+        for g in range(K_GROUPS):
+            nc.sync.dma_start(
+                out=w_words[:, g, :].bitcast(I32), in_=W1_words[g].rearrange("p n t -> p (n t)").bitcast(I32)
+            )
+        for quadrant in range(4):
+            nc.sync.dma_start(
+                out=w_scales[32 * quadrant : 32 * quadrant + 4, :, :].bitcast(I32),
+                in_=W1_scales[:, 4 * quadrant : 4 * quadrant + 4, :].rearrange("g r n -> r g n").bitcast(I32),
+            )
+
+        x_codes = {}
+        x_scales = {}
+
+        with tc.psum_pool(name="psum_t", bufs=4) as psum_t, tc.psum_pool(name="psum_x", bufs=4) as psum_x:
+            gain_shift_ps = psum_t.tile([P, P], BF16, tag="transposed")
+            nc.tensor.transpose(gain_shift_ps[:], gain_shift_rows[:], ident_bf16[:])
+            gain_shift = const.tile([P, 2 * CHANNEL_TILES], F32)
+            nc.vector.tensor_copy(out=gain_shift[:], in_=gain_shift_ps[:, 0 : 2 * CHANNEL_TILES])
+
+            for b in range(GRAPHS):
+                point_grouped = work.tile([P, PACK, P, PACK], BF16, align_bytes=64)
+                nc.vector.tensor_copy(
+                    out=point_grouped[:], in_=point_raw[b][:].rearrange("q t (pp tt) -> q tt pp t", tt=PACK)
+                )
+                point_codes = work.tile([P, FEATURES], U32, align_bytes=64)
+                point_scales = work.tile([P, FEATURES], U8, align_bytes=64)
+                nc.vector.quantize_mx(
+                    out=point_codes[:].bitcast(FP8X4),
+                    scales=point_scales[:],
+                    in_=point_grouped[:].rearrange("q tt pp t -> q (tt pp t)"),
+                )
+
+                for e in range(2):
+                    edge = edge_sb[b, e]
+                    diagonal_blocks = edge[:].rearrange("p r (c j) -> p (r c) j", j=P)[
+                        :, 0 : NODE_TILES * NODE_TILES : NODE_TILES + 1, :
+                    ]
+                    nc.vector.tensor_tensor(
+                        out=diagonal_blocks,
+                        in0=diagonal_blocks,
+                        in1=off_diagonal[:].unsqueeze(1).to_broadcast([P, NODE_TILES, P]),
+                        op=ALU.mult,
+                    )
+                    row_sum = small.tile([P, NODE_TILES], F32)
+                    for r in range(NODE_TILES):
+                        magnitudes = work.tile([P, NODES], BF16)
+                        nc.scalar.activation(
+                            out=magnitudes[:], in_=edge[:, r, :], func=ACT.Abs, accum_out=row_sum[:, r : r + 1]
+                        )
+                    row_scale = small.tile([P, NODE_TILES], F32)
+                    nc.vector.tensor_scalar_max(out=row_sum[:], in0=row_sum[:], scalar1=EPS_L1)
+                    nc.vector.reciprocal(out=row_scale[:], in_=row_sum[:])
+                    for r in range(NODE_TILES):
+                        nc.vector.tensor_scalar_mul(
+                            out=edge[:, r, :], in0=edge[:, r, :], scalar1=row_scale[:, r : r + 1]
+                        )
+
+                    edge_words = edge[:].bitcast(F32)
+                    edge_grouped = work.tile([P, NODES, PACK], BF16, align_bytes=64)
+                    grouped_words = edge_grouped[:].bitcast(F32)
+                    for half in range(2):
+                        transposed = psum_t.tile([P, 2, 2, P], F32, tag="transposed")
+                        for r in range(2):
+                            for u in range(2):
+                                nc.tensor.transpose(
+                                    transposed[:, r, u, :],
+                                    edge_words[:, 2 * half + r, u * P : (u + 1) * P],
+                                    ident_f32[:],
+                                )
+                        nc.vector.tensor_copy(
+                            out=grouped_words[:, half * 2 * P : (half + 1) * 2 * P, :].rearrange(
+                                "q (r n) u -> q r n u", r=2
+                            ),
+                            in_=transposed[:].rearrange("q r u n -> q r n u"),
+                        )
+                    edge_codes = work.tile([P, NODES], U32, align_bytes=64)
+                    edge_scales = work.tile([P, NODES], U8, align_bytes=64)
+                    nc.vector.quantize_mx(
+                        out=edge_codes[:].bitcast(FP8X4),
+                        scales=edge_scales[:],
+                        in_=edge_grouped[:].rearrange("q n t -> q (n t)"),
+                    )
+
+                    x_grouped = work.tile([P, NODES, PACK], BF16, align_bytes=64)
+                    for j in range(NODE_TILES):
+                        nodes = slice(j * P, (j + 1) * P)
+                        aggregate = psum_x.tile([P, PACK, P], F32)
+                        for tt in range(PACK):
+                            columns = slice(tt * P, (tt + 1) * P)
+                            nc.tensor.matmul_mx(
+                                out=aggregate[:, tt, :],
+                                lhsT=point_codes[:, columns].bitcast(FP8X4),
+                                lhsT_scale=point_scales[:, columns],
+                                rhs=edge_codes[:, nodes].bitcast(FP8X4),
+                                rhs_scale=edge_scales[:, nodes],
+                                start=True,
+                                stop=True,
+                            )
+                        nc.scalar.copy(out=x_grouped[:, nodes, :], in_=aggregate[:].rearrange("p t n -> p n t"))
+                    x_codes[b, e] = keep.tile([P, NODES], U32, align_bytes=64, name="x_codes_%d_%d" % (b, e))
+                    x_scales[b, e] = keep.tile([P, NODES], U8, align_bytes=64, name="x_scales_%d_%d" % (b, e))
+                    nc.vector.quantize_mx(
+                        out=x_codes[b, e][:].bitcast(FP8X4),
+                        scales=x_scales[b, e][:],
+                        in_=x_grouped[:].rearrange("p n t -> p (n t)"),
+                    )
+
+        with tc.psum_pool(name="psum_z", bufs=8, reuse_waits="tile") as psum_z:
+            for ot in range(CHANNEL_TILES):
+                channels = slice(ot * P, (ot + 1) * P)
+                stats = small.tile([P, GRAPHS, BN_STATS_DIM], F32)
+                z_banks = []
+                for b in range(GRAPHS):
+                    z = psum_z.tile([P, NODES], F32)
+                    for g in range(K_GROUPS):
+                        nc.tensor.matmul_mx(
+                            out=z[:],
+                            lhsT=w_words[:, g, channels].bitcast(FP8X4),
+                            lhsT_scale=w_scales[:, g, channels],
+                            rhs=x_codes[b, g][:].bitcast(FP8X4),
+                            rhs_scale=x_scales[b, g][:],
+                            start=(g == 0),
+                            stop=(g == K_GROUPS - 1),
+                        )
+                    nc.vector.bn_stats(out=stats[:, b, :], in_=z[:])
+                    z_banks.append(z)
+                mean_var = small.tile([P, 2], F32)
+                nc.vector.bn_aggr(out=mean_var[:], in_=stats[:].rearrange("p b s -> p (b s)"))
+                std = small.tile([P, 1], F32)
+                nc.scalar.activation(out=std[:], in_=mean_var[:, 1:2], func=ACT.Sqrt, bias=eps_bn[:])
+                rstd = small.tile([P, 1], F32)
+                nc.vector.reciprocal(out=rstd[:], in_=std[:])
+                y_scale = small.tile([P, 1], F32)
+                nc.vector.tensor_mul(out=y_scale[:], in0=rstd[:], in1=gain_shift[:, ot : ot + 1])
+                mean_scaled = small.tile([P, 1], F32)
+                nc.vector.tensor_mul(out=mean_scaled[:], in0=mean_var[:, 0:1], in1=y_scale[:])
+                y_shift = small.tile([P, 1], F32)
+                nc.vector.tensor_sub(
+                    out=y_shift[:],
+                    in0=gain_shift[:, CHANNEL_TILES + ot : CHANNEL_TILES + ot + 1],
+                    in1=mean_scaled[:],
+                )
+                y = work.tile([P, GRAPHS, NODES], F32)
+                for b in range(GRAPHS):
+                    nc.scalar.activation(
+                        out=y[:, b, :], in_=z_banks[b][:], func=ACT.Identity, scale=y_scale[:], bias=y_shift[:]
+                    )
+                y_flat = y[:].rearrange("p b n -> p (b n)")
+                nc.vector.scalar_tensor_tensor(
+                    out=y_flat, in0=y_flat, scalar=NEG_SLOPE, in1=y_flat, op0=ALU.mult, op1=ALU.max
+                )
+                nc.sync.dma_start(out=out[:, channels, :].rearrange("b p n -> p b n"), in_=y[:])

@@ -29,6 +29,9 @@ BN_STATS_DIM = 6
 FLOPS = 2 * GRAPHS * (2 * NODES * NODES * FEATURES + CHANNELS * CHANNELS * NODES)
 
 
+UNITS = 2 * GRAPHS
+
+
 def tile_yuyipointupdate_pa_kernel(
     tc, distribution_edge, instance_edge, point_node, W1_words, W1_scales, g1, b1, out
 ):
@@ -41,6 +44,8 @@ def tile_yuyipointupdate_pa_kernel(
         keep = ctx.enter_context(tc.tile_pool(name="keep", bufs=1))
         work = ctx.enter_context(tc.tile_pool(name="work", bufs=3))
         small = ctx.enter_context(tc.tile_pool(name="small", bufs=4))
+        psum = ctx.enter_context(tc.psum_pool(name="psum", bufs=8))
+        ctx.enter_context(tc.manual_schedule())
 
         ident_f32 = const.tile([P, P], F32)
         make_identity(nc, ident_f32[:])
@@ -61,8 +66,8 @@ def tile_yuyipointupdate_pa_kernel(
         point_raw = {}
         for b in range(GRAPHS):
             for e in range(2):
-                edge_sb[b, e] = inputs.tile([P, NODE_TILES, NODES], BF16, name="edge_%d_%d" % (b, e))
-                nc.sync.dma_start(out=edge_sb[b, e][:], in_=edges[e][b].rearrange("(r p) m -> p r m", p=P))
+                edge_sb[2 * b + e] = inputs.tile([P, NODE_TILES, NODES], BF16, name="edge_%d" % (2 * b + e))
+                nc.sync.dma_start(out=edge_sb[2 * b + e][:], in_=edges[e][b].rearrange("(r p) m -> p r m", p=P))
             point_raw[b] = inputs.tile([P, PACK, FEATURES], BF16, name="point_%d" % b)
             nc.sync.dma_start(
                 out=point_raw[b][:].rearrange("q (u e) d -> q u e d", u=2),
@@ -83,145 +88,224 @@ def tile_yuyipointupdate_pa_kernel(
                 in_=W1_scales[:, 4 * quadrant : 4 * quadrant + 4, :].rearrange("g r n -> r g n").bitcast(I32),
             )
 
+        row_sum = {}
+        transposed = {}
+        edge_grouped = {}
+        edge_codes = {}
+        edge_scales = {}
+        point_codes = {}
+        point_scales = {}
+        x_grouped = {}
         x_codes = {}
         x_scales = {}
 
-        with tc.psum_pool(name="psum_t", bufs=4) as psum_t, tc.psum_pool(name="psum_x", bufs=4) as psum_x:
-            gain_shift_ps = psum_t.tile([P, P], BF16, tag="transposed")
-            nc.tensor.transpose(gain_shift_ps[:], gain_shift_rows[:], ident_bf16[:])
-            gain_shift = const.tile([P, 2 * CHANNEL_TILES], F32)
-            nc.vector.tensor_copy(out=gain_shift[:], in_=gain_shift_ps[:, 0 : 2 * CHANNEL_TILES])
+        def quantise_points(b):
+            point_grouped = work.tile([P, PACK, P, PACK], BF16, align_bytes=64)
+            nc.vector.tensor_copy(
+                out=point_grouped[:], in_=point_raw[b][:].rearrange("q t (pp tt) -> q tt pp t", tt=PACK)
+            )
+            point_codes[b] = work.tile([P, FEATURES], U32, align_bytes=64, name="point_codes_%d" % b, tag="point_codes")
+            point_scales[b] = work.tile([P, FEATURES], U8, align_bytes=64, name="point_scales_%d" % b, tag="point_scales")
+            nc.vector.quantize_mx(
+                out=point_codes[b][:].bitcast(FP8X4),
+                scales=point_scales[b][:],
+                in_=point_grouped[:].rearrange("q tt pp t -> q (tt pp t)"),
+            )
 
-            for b in range(GRAPHS):
-                point_grouped = work.tile([P, PACK, P, PACK], BF16, align_bytes=64)
+        def mask_diagonal(unit):
+            diagonal_blocks = edge_sb[unit][:].rearrange("p r (c j) -> p (r c) j", j=P)[
+                :, 0 : NODE_TILES * NODE_TILES : NODE_TILES + 1, :
+            ]
+            nc.vector.tensor_tensor(
+                out=diagonal_blocks,
+                in0=diagonal_blocks,
+                in1=off_diagonal[:].unsqueeze(1).to_broadcast([P, NODE_TILES, P]),
+                op=ALU.mult,
+            )
+
+        def sum_rows(unit):
+            row_sum[unit] = small.tile([P, NODE_TILES], F32, name="row_sum_%d" % unit, tag="row_sum")
+            for r in range(NODE_TILES):
+                magnitudes = work.tile([P, NODES], BF16)
+                nc.scalar.activation(
+                    out=magnitudes[:],
+                    in_=edge_sb[unit][:, r, :],
+                    func=ACT.Abs,
+                    accum_out=row_sum[unit][:, r : r + 1],
+                )
+
+        def divide_rows(unit):
+            row_scale = small.tile([P, NODE_TILES], F32)
+            nc.vector.tensor_scalar_max(out=row_sum[unit][:], in0=row_sum[unit][:], scalar1=EPS_L1)
+            nc.vector.reciprocal(out=row_scale[:], in_=row_sum[unit][:])
+            for r in range(NODE_TILES):
+                nc.vector.tensor_scalar_mul(
+                    out=edge_sb[unit][:, r, :], in0=edge_sb[unit][:, r, :], scalar1=row_scale[:, r : r + 1]
+                )
+
+        def transpose_edges(unit):
+            edge_words = edge_sb[unit][:].bitcast(F32)
+            for half in range(2):
+                transposed[unit, half] = psum.tile([P, 2, 2, P], F32, name="transposed_%d_%d" % (unit, half), tag="bank")
+                for r in range(2):
+                    for u in range(2):
+                        nc.tensor.transpose(
+                            transposed[unit, half][:, r, u, :],
+                            edge_words[:, 2 * half + r, u * P : (u + 1) * P],
+                            ident_f32[:],
+                        )
+
+        def collect_transposed(unit):
+            edge_grouped[unit] = work.tile([P, NODES, PACK], BF16, align_bytes=64, name="edge_grouped_%d" % unit, tag="edge_grouped")
+            grouped_words = edge_grouped[unit][:].bitcast(F32)
+            for half in range(2):
                 nc.vector.tensor_copy(
-                    out=point_grouped[:], in_=point_raw[b][:].rearrange("q t (pp tt) -> q tt pp t", tt=PACK)
-                )
-                point_codes = work.tile([P, FEATURES], U32, align_bytes=64)
-                point_scales = work.tile([P, FEATURES], U8, align_bytes=64)
-                nc.vector.quantize_mx(
-                    out=point_codes[:].bitcast(FP8X4),
-                    scales=point_scales[:],
-                    in_=point_grouped[:].rearrange("q tt pp t -> q (tt pp t)"),
+                    out=grouped_words[:, half * 2 * P : (half + 1) * 2 * P, :].rearrange("q (r n) u -> q r n u", r=2),
+                    in_=transposed[unit, half][:].rearrange("q r u n -> q r n u"),
                 )
 
-                for e in range(2):
-                    edge = edge_sb[b, e]
-                    diagonal_blocks = edge[:].rearrange("p r (c j) -> p (r c) j", j=P)[
-                        :, 0 : NODE_TILES * NODE_TILES : NODE_TILES + 1, :
-                    ]
-                    nc.vector.tensor_tensor(
-                        out=diagonal_blocks,
-                        in0=diagonal_blocks,
-                        in1=off_diagonal[:].unsqueeze(1).to_broadcast([P, NODE_TILES, P]),
-                        op=ALU.mult,
-                    )
-                    row_sum = small.tile([P, NODE_TILES], F32)
-                    for r in range(NODE_TILES):
-                        magnitudes = work.tile([P, NODES], BF16)
-                        nc.scalar.activation(
-                            out=magnitudes[:], in_=edge[:, r, :], func=ACT.Abs, accum_out=row_sum[:, r : r + 1]
-                        )
-                    row_scale = small.tile([P, NODE_TILES], F32)
-                    nc.vector.tensor_scalar_max(out=row_sum[:], in0=row_sum[:], scalar1=EPS_L1)
-                    nc.vector.reciprocal(out=row_scale[:], in_=row_sum[:])
-                    for r in range(NODE_TILES):
-                        nc.vector.tensor_scalar_mul(
-                            out=edge[:, r, :], in0=edge[:, r, :], scalar1=row_scale[:, r : r + 1]
-                        )
+        def quantise_edges(unit):
+            edge_codes[unit] = work.tile([P, NODES], U32, align_bytes=64, name="edge_codes_%d" % unit, tag="edge_codes")
+            edge_scales[unit] = work.tile([P, NODES], U8, align_bytes=64, name="edge_scales_%d" % unit, tag="edge_scales")
+            nc.vector.quantize_mx(
+                out=edge_codes[unit][:].bitcast(FP8X4),
+                scales=edge_scales[unit][:],
+                in_=edge_grouped[unit][:].rearrange("q n t -> q (n t)"),
+            )
 
-                    edge_words = edge[:].bitcast(F32)
-                    edge_grouped = work.tile([P, NODES, PACK], BF16, align_bytes=64)
-                    grouped_words = edge_grouped[:].bitcast(F32)
-                    for half in range(2):
-                        transposed = psum_t.tile([P, 2, 2, P], F32, tag="transposed")
-                        for r in range(2):
-                            for u in range(2):
-                                nc.tensor.transpose(
-                                    transposed[:, r, u, :],
-                                    edge_words[:, 2 * half + r, u * P : (u + 1) * P],
-                                    ident_f32[:],
-                                )
-                        nc.vector.tensor_copy(
-                            out=grouped_words[:, half * 2 * P : (half + 1) * 2 * P, :].rearrange(
-                                "q (r n) u -> q r n u", r=2
-                            ),
-                            in_=transposed[:].rearrange("q r u n -> q r n u"),
-                        )
-                    edge_codes = work.tile([P, NODES], U32, align_bytes=64)
-                    edge_scales = work.tile([P, NODES], U8, align_bytes=64)
-                    nc.vector.quantize_mx(
-                        out=edge_codes[:].bitcast(FP8X4),
-                        scales=edge_scales[:],
-                        in_=edge_grouped[:].rearrange("q n t -> q (n t)"),
+        def aggregate(unit):
+            b = unit // 2
+            x_grouped[unit] = work.tile([P, NODES, PACK], BF16, align_bytes=64, name="x_grouped_%d" % unit, tag="x_grouped")
+            for j in range(NODE_TILES):
+                nodes = slice(j * P, (j + 1) * P)
+                aggregated = psum.tile([P, PACK, P], F32, tag="bank")
+                for tt in range(PACK):
+                    columns = slice(tt * P, (tt + 1) * P)
+                    nc.tensor.matmul_mx(
+                        out=aggregated[:, tt, :],
+                        lhsT=point_codes[b][:, columns].bitcast(FP8X4),
+                        lhsT_scale=point_scales[b][:, columns],
+                        rhs=edge_codes[unit][:, nodes].bitcast(FP8X4),
+                        rhs_scale=edge_scales[unit][:, nodes],
+                        start=True,
+                        stop=True,
                     )
+                nc.scalar.copy(out=x_grouped[unit][:, nodes, :], in_=aggregated[:].rearrange("p t n -> p n t"))
 
-                    x_grouped = work.tile([P, NODES, PACK], BF16, align_bytes=64)
-                    for j in range(NODE_TILES):
-                        nodes = slice(j * P, (j + 1) * P)
-                        aggregate = psum_x.tile([P, PACK, P], F32)
-                        for tt in range(PACK):
-                            columns = slice(tt * P, (tt + 1) * P)
-                            nc.tensor.matmul_mx(
-                                out=aggregate[:, tt, :],
-                                lhsT=point_codes[:, columns].bitcast(FP8X4),
-                                lhsT_scale=point_scales[:, columns],
-                                rhs=edge_codes[:, nodes].bitcast(FP8X4),
-                                rhs_scale=edge_scales[:, nodes],
-                                start=True,
-                                stop=True,
-                            )
-                        nc.scalar.copy(out=x_grouped[:, nodes, :], in_=aggregate[:].rearrange("p t n -> p n t"))
-                    x_codes[b, e] = keep.tile([P, NODES], U32, align_bytes=64, name="x_codes_%d_%d" % (b, e))
-                    x_scales[b, e] = keep.tile([P, NODES], U8, align_bytes=64, name="x_scales_%d_%d" % (b, e))
-                    nc.vector.quantize_mx(
-                        out=x_codes[b, e][:].bitcast(FP8X4),
-                        scales=x_scales[b, e][:],
-                        in_=x_grouped[:].rearrange("p n t -> p (n t)"),
+        def quantise_x(unit):
+            x_codes[unit] = keep.tile([P, NODES], U32, align_bytes=64, name="x_codes_%d" % unit)
+            x_scales[unit] = keep.tile([P, NODES], U8, align_bytes=64, name="x_scales_%d" % unit)
+            nc.vector.quantize_mx(
+                out=x_codes[unit][:].bitcast(FP8X4),
+                scales=x_scales[unit][:],
+                in_=x_grouped[unit][:].rearrange("p n t -> p (n t)"),
+            )
+
+        mask_diagonal(0)
+        sum_rows(0)
+        mask_diagonal(1)
+        sum_rows(1)
+        quantise_points(0)
+        divide_rows(0)
+        transpose_edges(0)
+        mask_diagonal(2)
+        collect_transposed(0)
+        for i in range(UNITS):
+            if i + 1 < UNITS:
+                divide_rows(i + 1)
+                transpose_edges(i + 1)
+            quantise_edges(i)
+            if i + 2 < UNITS:
+                sum_rows(i + 2)
+            aggregate(i)
+            if i + 3 < UNITS:
+                mask_diagonal(i + 3)
+            if i + 1 < UNITS:
+                collect_transposed(i + 1)
+            if i >= 1:
+                quantise_x(i - 1)
+            if i % 2 == 1 and i + 1 < UNITS:
+                quantise_points((i + 1) // 2)
+        quantise_x(UNITS - 1)
+
+        gain_shift_ps = psum.tile([P, P], BF16, tag="bank")
+        nc.tensor.transpose(gain_shift_ps[:], gain_shift_rows[:], ident_bf16[:])
+        gain_shift = const.tile([P, 2 * CHANNEL_TILES], F32)
+        nc.vector.tensor_copy(out=gain_shift[:], in_=gain_shift_ps[:, 0 : 2 * CHANNEL_TILES])
+
+        z_banks = {}
+        mean_var = {}
+        std = {}
+        y_scale = {}
+        y_shift = {}
+        y = {}
+
+        def convolve(ot):
+            channels = slice(ot * P, (ot + 1) * P)
+            stats = small.tile([P, GRAPHS, BN_STATS_DIM], F32)
+            for b in range(GRAPHS):
+                z_banks[ot, b] = psum.tile([P, NODES], F32, name="z_%d_%d" % (ot, b), tag="bank")
+                for g in range(K_GROUPS):
+                    nc.tensor.matmul_mx(
+                        out=z_banks[ot, b][:],
+                        lhsT=w_words[:, g, channels].bitcast(FP8X4),
+                        lhsT_scale=w_scales[:, g, channels],
+                        rhs=x_codes[2 * b + g][:].bitcast(FP8X4),
+                        rhs_scale=x_scales[2 * b + g][:],
+                        start=(g == 0),
+                        stop=(g == K_GROUPS - 1),
                     )
+                nc.vector.bn_stats(out=stats[:, b, :], in_=z_banks[ot, b][:])
+            mean_var[ot] = small.tile([P, 2], F32, name="mean_var_%d" % ot, tag="mean_var")
+            nc.vector.bn_aggr(out=mean_var[ot][:], in_=stats[:].rearrange("p b s -> p (b s)"))
 
-        with tc.psum_pool(name="psum_z", bufs=8, reuse_waits="tile") as psum_z:
-            for ot in range(CHANNEL_TILES):
-                channels = slice(ot * P, (ot + 1) * P)
-                stats = small.tile([P, GRAPHS, BN_STATS_DIM], F32)
-                z_banks = []
-                for b in range(GRAPHS):
-                    z = psum_z.tile([P, NODES], F32)
-                    for g in range(K_GROUPS):
-                        nc.tensor.matmul_mx(
-                            out=z[:],
-                            lhsT=w_words[:, g, channels].bitcast(FP8X4),
-                            lhsT_scale=w_scales[:, g, channels],
-                            rhs=x_codes[b, g][:].bitcast(FP8X4),
-                            rhs_scale=x_scales[b, g][:],
-                            start=(g == 0),
-                            stop=(g == K_GROUPS - 1),
-                        )
-                    nc.vector.bn_stats(out=stats[:, b, :], in_=z[:])
-                    z_banks.append(z)
-                mean_var = small.tile([P, 2], F32)
-                nc.vector.bn_aggr(out=mean_var[:], in_=stats[:].rearrange("p b s -> p (b s)"))
-                std = small.tile([P, 1], F32)
-                nc.scalar.activation(out=std[:], in_=mean_var[:, 1:2], func=ACT.Sqrt, bias=eps_bn[:])
-                rstd = small.tile([P, 1], F32)
-                nc.vector.reciprocal(out=rstd[:], in_=std[:])
-                y_scale = small.tile([P, 1], F32)
-                nc.vector.tensor_mul(out=y_scale[:], in0=rstd[:], in1=gain_shift[:, ot : ot + 1])
-                mean_scaled = small.tile([P, 1], F32)
-                nc.vector.tensor_mul(out=mean_scaled[:], in0=mean_var[:, 0:1], in1=y_scale[:])
-                y_shift = small.tile([P, 1], F32)
-                nc.vector.tensor_sub(
-                    out=y_shift[:],
-                    in0=gain_shift[:, CHANNEL_TILES + ot : CHANNEL_TILES + ot + 1],
-                    in1=mean_scaled[:],
+        def deviation(ot):
+            std[ot] = small.tile([P, 1], F32, name="std_%d" % ot, tag="std")
+            nc.scalar.activation(out=std[ot][:], in_=mean_var[ot][:, 1:2], func=ACT.Sqrt, bias=eps_bn[:])
+
+        def affine(ot):
+            rstd = small.tile([P, 1], F32)
+            nc.vector.reciprocal(out=rstd[:], in_=std[ot][:])
+            y_scale[ot] = small.tile([P, 1], F32, name="y_scale_%d" % ot, tag="y_scale")
+            nc.vector.tensor_mul(out=y_scale[ot][:], in0=rstd[:], in1=gain_shift[:, ot : ot + 1])
+            mean_scaled = small.tile([P, 1], F32)
+            nc.vector.tensor_mul(out=mean_scaled[:], in0=mean_var[ot][:, 0:1], in1=y_scale[ot][:])
+            y_shift[ot] = small.tile([P, 1], F32, name="y_shift_%d" % ot, tag="y_shift")
+            nc.vector.tensor_sub(
+                out=y_shift[ot][:], in0=gain_shift[:, CHANNEL_TILES + ot : CHANNEL_TILES + ot + 1], in1=mean_scaled[:]
+            )
+
+        def normalise(ot):
+            y[ot] = work.tile([P, GRAPHS, NODES], F32, name="y_%d" % ot, tag="y")
+            for b in range(GRAPHS):
+                nc.scalar.activation(
+                    out=y[ot][:, b, :],
+                    in_=z_banks[ot, b][:],
+                    func=ACT.Identity,
+                    scale=y_scale[ot][:],
+                    bias=y_shift[ot][:],
                 )
-                y = work.tile([P, GRAPHS, NODES], F32)
-                for b in range(GRAPHS):
-                    nc.scalar.activation(
-                        out=y[:, b, :], in_=z_banks[b][:], func=ACT.Identity, scale=y_scale[:], bias=y_shift[:]
-                    )
-                y_flat = y[:].rearrange("p b n -> p (b n)")
+
+        def leaky_relu_and_store(ot):
+            channels = slice(ot * P, (ot + 1) * P)
+            for half in range(2):
+                graphs = slice(2 * half, 2 * half + 2)
+                y_half = y[ot][:, graphs, :].rearrange("p b n -> p (b n)")
                 nc.vector.scalar_tensor_tensor(
-                    out=y_flat, in0=y_flat, scalar=NEG_SLOPE, in1=y_flat, op0=ALU.mult, op1=ALU.max
+                    out=y_half, in0=y_half, scalar=NEG_SLOPE, in1=y_half, op0=ALU.mult, op1=ALU.max
                 )
-                nc.sync.dma_start(out=out[:, channels, :].rearrange("b p n -> p b n"), in_=y[:])
+                nc.sync.dma_start(
+                    out=out[graphs, channels, :].rearrange("b p n -> p b n"), in_=y[ot][:, graphs, :]
+                )
+
+        convolve(0)
+        deviation(0)
+        affine(0)
+        for ot in range(CHANNEL_TILES):
+            normalise(ot)
+            if ot + 1 < CHANNEL_TILES:
+                convolve(ot + 1)
+                deviation(ot + 1)
+            leaky_relu_and_store(ot)
+            if ot + 1 < CHANNEL_TILES:
+                affine(ot + 1)

@@ -55,13 +55,17 @@ def tile_yuyipointupdate_pa_kernel(
         nc.vector.tensor_scalar(
             out=off_diagonal[:], in0=ident_bf16[:], scalar1=-1.0, scalar2=1.0, op0=ALU.mult, op1=ALU.add
         )
-        eps_bn = const.tile([P, 1], F32)
-        nc.vector.memset(eps_bn[:], EPS_BN)
+        minus_half = const.tile([P, 1], F32)
+        nc.vector.memset(minus_half[:], -0.5)
         gain_shift_rows = const.tile([P, P], BF16)
         nc.vector.memset(gain_shift_rows[:], 0.0)
         w_scales = keep.tile([P, K_GROUPS, CHANNELS], U8, align_bytes=64)
         nc.vector.memset(w_scales[:].rearrange("p g n -> p (g n)").bitcast(I32), 0)
 
+        nc.sync.dma_start(out=gain_shift_rows[0:CHANNEL_TILES, :], in_=g1.rearrange("(t p) -> t p", p=P))
+        nc.sync.dma_start(
+            out=gain_shift_rows[CHANNEL_TILES : 2 * CHANNEL_TILES, :], in_=b1.rearrange("(t p) -> t p", p=P)
+        )
         edge_sb = {}
         point_raw = {}
         for b in range(GRAPHS):
@@ -73,10 +77,6 @@ def tile_yuyipointupdate_pa_kernel(
                 out=point_raw[b][:].rearrange("q (u e) d -> q u e d", u=2),
                 in_=point_node[b].rearrange("(u q e) d -> q u e d", u=2, e=2),
             )
-        nc.sync.dma_start(out=gain_shift_rows[0:CHANNEL_TILES, :], in_=g1.rearrange("(t p) -> t p", p=P))
-        nc.sync.dma_start(
-            out=gain_shift_rows[CHANNEL_TILES : 2 * CHANNEL_TILES, :], in_=b1.rearrange("(t p) -> t p", p=P)
-        )
         w_words = keep.tile([P, K_GROUPS, CHANNELS], U32, align_bytes=64)
         for g in range(K_GROUPS):
             nc.sync.dma_start(
@@ -88,7 +88,9 @@ def tile_yuyipointupdate_pa_kernel(
                 in_=W1_scales[:, 4 * quadrant : 4 * quadrant + 4, :].rearrange("g r n -> r g n").bitcast(I32),
             )
 
+        point_grouped = {}
         row_sum = {}
+        row_scale = {}
         transposed = {}
         edge_grouped = {}
         edge_codes = {}
@@ -99,17 +101,19 @@ def tile_yuyipointupdate_pa_kernel(
         x_codes = {}
         x_scales = {}
 
-        def quantise_points(b):
-            point_grouped = work.tile([P, PACK, P, PACK], BF16, align_bytes=64)
+        def regroup_points(b):
+            point_grouped[b] = work.tile([P, PACK, P, PACK], BF16, align_bytes=64, name="point_grouped_%d" % b, tag="point_grouped")
             nc.vector.tensor_copy(
-                out=point_grouped[:], in_=point_raw[b][:].rearrange("q t (pp tt) -> q tt pp t", tt=PACK)
+                out=point_grouped[b][:], in_=point_raw[b][:].rearrange("q t (pp tt) -> q tt pp t", tt=PACK)
             )
+
+        def quantise_points(b):
             point_codes[b] = work.tile([P, FEATURES], U32, align_bytes=64, name="point_codes_%d" % b, tag="point_codes")
             point_scales[b] = work.tile([P, FEATURES], U8, align_bytes=64, name="point_scales_%d" % b, tag="point_scales")
             nc.vector.quantize_mx(
                 out=point_codes[b][:].bitcast(FP8X4),
                 scales=point_scales[b][:],
-                in_=point_grouped[:].rearrange("q tt pp t -> q (tt pp t)"),
+                in_=point_grouped[b][:].rearrange("q tt pp t -> q (tt pp t)"),
             )
 
         def mask_diagonal(unit):
@@ -134,13 +138,17 @@ def tile_yuyipointupdate_pa_kernel(
                     accum_out=row_sum[unit][:, r : r + 1],
                 )
 
-        def divide_rows(unit):
-            row_scale = small.tile([P, NODE_TILES], F32)
+        def clamp_sums(unit):
             nc.vector.tensor_scalar_max(out=row_sum[unit][:], in0=row_sum[unit][:], scalar1=EPS_L1)
-            nc.vector.reciprocal(out=row_scale[:], in_=row_sum[unit][:])
+
+        def invert_sums(unit):
+            row_scale[unit] = small.tile([P, NODE_TILES], F32, name="row_scale_%d" % unit, tag="row_scale")
+            nc.vector.reciprocal(out=row_scale[unit][:], in_=row_sum[unit][:])
+
+        def scale_rows(unit):
             for r in range(NODE_TILES):
                 nc.vector.tensor_scalar_mul(
-                    out=edge_sb[unit][:, r, :], in0=edge_sb[unit][:, r, :], scalar1=row_scale[:, r : r + 1]
+                    out=edge_sb[unit][:, r, :], in0=edge_sb[unit][:, r, :], scalar1=row_scale[unit][:, r : r + 1]
                 )
 
         def transpose_edges(unit):
@@ -155,14 +163,14 @@ def tile_yuyipointupdate_pa_kernel(
                             ident_f32[:],
                         )
 
-        def collect_transposed(unit):
-            edge_grouped[unit] = work.tile([P, NODES, PACK], BF16, align_bytes=64, name="edge_grouped_%d" % unit, tag="edge_grouped")
+        def collect_transposed(unit, half):
+            if half == 0:
+                edge_grouped[unit] = work.tile([P, NODES, PACK], BF16, align_bytes=64, name="edge_grouped_%d" % unit, tag="edge_grouped")
             grouped_words = edge_grouped[unit][:].bitcast(F32)
-            for half in range(2):
-                nc.vector.tensor_copy(
-                    out=grouped_words[:, half * 2 * P : (half + 1) * 2 * P, :].rearrange("q (r n) u -> q r n u", r=2),
-                    in_=transposed[unit, half][:].rearrange("q r u n -> q r n u"),
-                )
+            nc.vector.tensor_copy(
+                out=grouped_words[:, half * 2 * P : (half + 1) * 2 * P, :].rearrange("q (r n) u -> q r n u", r=2),
+                in_=transposed[unit, half][:].rearrange("q r u n -> q r n u"),
+            )
 
         def quantise_edges(unit):
             edge_codes[unit] = work.tile([P, NODES], U32, align_bytes=64, name="edge_codes_%d" % unit, tag="edge_codes")
@@ -201,41 +209,53 @@ def tile_yuyipointupdate_pa_kernel(
                 in_=x_grouped[unit][:].rearrange("p n t -> p (n t)"),
             )
 
-        mask_diagonal(0)
-        sum_rows(0)
-        mask_diagonal(1)
-        sum_rows(1)
-        quantise_points(0)
-        divide_rows(0)
-        transpose_edges(0)
-        mask_diagonal(2)
-        collect_transposed(0)
-        for i in range(UNITS):
-            if i + 1 < UNITS:
-                divide_rows(i + 1)
-                transpose_edges(i + 1)
-            quantise_edges(i)
-            if i + 2 < UNITS:
-                sum_rows(i + 2)
-            aggregate(i)
-            if i + 3 < UNITS:
-                mask_diagonal(i + 3)
-            if i + 1 < UNITS:
-                collect_transposed(i + 1)
-            if i >= 1:
-                quantise_x(i - 1)
-            if i % 2 == 1 and i + 1 < UNITS:
-                quantise_points((i + 1) // 2)
-        quantise_x(UNITS - 1)
-
         gain_shift_ps = psum.tile([P, P], BF16, tag="bank")
         nc.tensor.transpose(gain_shift_ps[:], gain_shift_rows[:], ident_bf16[:])
         gain_shift = const.tile([P, 2 * CHANNEL_TILES], F32)
         nc.vector.tensor_copy(out=gain_shift[:], in_=gain_shift_ps[:, 0 : 2 * CHANNEL_TILES])
 
+        def prepare(unit):
+            if unit < UNITS:
+                clamp_sums(unit)
+            if 1 <= unit <= UNITS:
+                collect_transposed(unit - 1, 0)
+            if unit < UNITS:
+                invert_sums(unit)
+            if 1 <= unit <= UNITS:
+                collect_transposed(unit - 1, 1)
+            if unit < UNITS:
+                scale_rows(unit)
+                transpose_edges(unit)
+
+        mask_diagonal(0)
+        sum_rows(0)
+        mask_diagonal(1)
+        sum_rows(1)
+        regroup_points(0)
+        mask_diagonal(2)
+        sum_rows(2)
+        prepare(0)
+        quantise_points(0)
+        mask_diagonal(3)
+        prepare(1)
+        for i in range(UNITS):
+            quantise_edges(i)
+            if i + 3 < UNITS:
+                sum_rows(i + 3)
+            aggregate(i)
+            prepare(i + 2)
+            if i >= 1:
+                quantise_x(i - 1)
+            if i + 4 < UNITS:
+                mask_diagonal(i + 4)
+            if i + 2 < UNITS and i % 2 == 0:
+                regroup_points(i // 2 + 1)
+            if i + 1 < UNITS and i % 2 == 1:
+                quantise_points(i // 2 + 1)
+        quantise_x(UNITS - 1)
+
         z_banks = {}
         mean_var = {}
-        std = {}
         y_scale = {}
         y_shift = {}
         y = {}
@@ -259,19 +279,17 @@ def tile_yuyipointupdate_pa_kernel(
             mean_var[ot] = small.tile([P, 2], F32, name="mean_var_%d" % ot, tag="mean_var")
             nc.vector.bn_aggr(out=mean_var[ot][:], in_=stats[:].rearrange("p b s -> p (b s)"))
 
-        def deviation(ot):
-            std[ot] = small.tile([P, 1], F32, name="std_%d" % ot, tag="std")
-            nc.scalar.activation(out=std[ot][:], in_=mean_var[ot][:, 1:2], func=ACT.Sqrt, bias=eps_bn[:])
-
         def affine(ot):
+            variance_eps = small.tile([P, 1], F32)
+            nc.gpsimd.tensor_scalar_add(out=variance_eps[:], in0=mean_var[ot][:, 1:2], scalar1=EPS_BN)
             rstd = small.tile([P, 1], F32)
-            nc.vector.reciprocal(out=rstd[:], in_=std[ot][:])
+            nc.gpsimd.tensor_tensor(out=rstd[:], in0=variance_eps[:], in1=minus_half[:], op=ALU.pow)
             y_scale[ot] = small.tile([P, 1], F32, name="y_scale_%d" % ot, tag="y_scale")
-            nc.vector.tensor_mul(out=y_scale[ot][:], in0=rstd[:], in1=gain_shift[:, ot : ot + 1])
+            nc.gpsimd.tensor_mul(out=y_scale[ot][:], in0=rstd[:], in1=gain_shift[:, ot : ot + 1])
             mean_scaled = small.tile([P, 1], F32)
-            nc.vector.tensor_mul(out=mean_scaled[:], in0=mean_var[ot][:, 0:1], in1=y_scale[ot][:])
+            nc.gpsimd.tensor_mul(out=mean_scaled[:], in0=mean_var[ot][:, 0:1], in1=y_scale[ot][:])
             y_shift[ot] = small.tile([P, 1], F32, name="y_shift_%d" % ot, tag="y_shift")
-            nc.vector.tensor_sub(
+            nc.gpsimd.tensor_sub(
                 out=y_shift[ot][:], in0=gain_shift[:, CHANNEL_TILES + ot : CHANNEL_TILES + ot + 1], in1=mean_scaled[:]
             )
 
@@ -299,13 +317,10 @@ def tile_yuyipointupdate_pa_kernel(
                 )
 
         convolve(0)
-        deviation(0)
         affine(0)
         for ot in range(CHANNEL_TILES):
             normalise(ot)
             if ot + 1 < CHANNEL_TILES:
                 convolve(ot + 1)
-                deviation(ot + 1)
-            leaky_relu_and_store(ot)
-            if ot + 1 < CHANNEL_TILES:
                 affine(ot + 1)
+            leaky_relu_and_store(ot)

@@ -62,10 +62,6 @@ def tile_yuyipointupdate_pa_kernel(
         w_scales = keep.tile([P, K_GROUPS, CHANNELS], U8, align_bytes=64)
         nc.vector.memset(w_scales[:].rearrange("p g n -> p (g n)").bitcast(I32), 0)
 
-        nc.sync.dma_start(out=gain_shift_rows[0:CHANNEL_TILES, :], in_=g1.rearrange("(t p) -> t p", p=P))
-        nc.sync.dma_start(
-            out=gain_shift_rows[CHANNEL_TILES : 2 * CHANNEL_TILES, :], in_=b1.rearrange("(t p) -> t p", p=P)
-        )
         edge_sb = {}
         point_raw = {}
         for b in range(GRAPHS):
@@ -77,6 +73,10 @@ def tile_yuyipointupdate_pa_kernel(
                 out=point_raw[b][:].rearrange("q (u e) d -> q u e d", u=2),
                 in_=point_node[b].rearrange("(u q e) d -> q u e d", u=2, e=2),
             )
+        nc.sync.dma_start(out=gain_shift_rows[0:CHANNEL_TILES, :], in_=g1.rearrange("(t p) -> t p", p=P))
+        nc.sync.dma_start(
+            out=gain_shift_rows[CHANNEL_TILES : 2 * CHANNEL_TILES, :], in_=b1.rearrange("(t p) -> t p", p=P)
+        )
         w_words = keep.tile([P, K_GROUPS, CHANNELS], U32, align_bytes=64)
         for g in range(K_GROUPS):
             nc.sync.dma_start(
@@ -103,9 +103,11 @@ def tile_yuyipointupdate_pa_kernel(
 
         def regroup_points(b):
             point_grouped[b] = work.tile([P, PACK, P, PACK], BF16, align_bytes=64, name="point_grouped_%d" % b, tag="point_grouped")
-            nc.vector.tensor_copy(
-                out=point_grouped[b][:], in_=point_raw[b][:].rearrange("q t (pp tt) -> q tt pp t", tt=PACK)
-            )
+            by_word = point_raw[b][:].rearrange("q t (pp tt) -> q tt pp t", tt=PACK)
+            if b == 0:
+                nc.vector.tensor_copy(out=point_grouped[b][:], in_=by_word)
+            else:
+                nc.scalar.copy(out=point_grouped[b][:], in_=by_word)
 
         def quantise_points(b):
             point_codes[b] = work.tile([P, FEATURES], U32, align_bytes=64, name="point_codes_%d" % b, tag="point_codes")
@@ -209,23 +211,27 @@ def tile_yuyipointupdate_pa_kernel(
                 in_=x_grouped[unit][:].rearrange("p n t -> p (n t)"),
             )
 
-        gain_shift_ps = psum.tile([P, P], BF16, tag="bank")
-        nc.tensor.transpose(gain_shift_ps[:], gain_shift_rows[:], ident_bf16[:])
-        gain_shift = const.tile([P, 2 * CHANNEL_TILES], F32)
-        nc.vector.tensor_copy(out=gain_shift[:], in_=gain_shift_ps[:, 0 : 2 * CHANNEL_TILES])
+        stats = keep.tile([P, CHANNEL_TILES, GRAPHS, BN_STATS_DIM], F32)
 
-        def prepare(unit):
-            if unit < UNITS:
-                clamp_sums(unit)
-            if 1 <= unit <= UNITS:
-                collect_transposed(unit - 1, 0)
-            if unit < UNITS:
-                invert_sums(unit)
-            if 1 <= unit <= UNITS:
-                collect_transposed(unit - 1, 1)
-            if unit < UNITS:
-                scale_rows(unit)
-                transpose_edges(unit)
+        def convolve(ot, b):
+            channels = slice(ot * P, (ot + 1) * P)
+            z = psum.tile([P, NODES], F32, name="z_%d_%d" % (ot, b), tag="bank")
+            for g in range(K_GROUPS):
+                nc.tensor.matmul_mx(
+                    out=z[:],
+                    lhsT=w_words[:, g, channels].bitcast(FP8X4),
+                    lhsT_scale=w_scales[:, g, channels],
+                    rhs=x_codes[2 * b + g][:].bitcast(FP8X4),
+                    rhs_scale=x_scales[2 * b + g][:],
+                    start=(g == 0),
+                    stop=(g == K_GROUPS - 1),
+                )
+            return z
+
+        def survey(b, channel_tiles):
+            for ot in channel_tiles:
+                z = convolve(ot, b)
+                nc.vector.bn_stats(out=stats[:, ot, b, :], in_=z[:])
 
         mask_diagonal(0)
         sum_rows(0)
@@ -234,25 +240,52 @@ def tile_yuyipointupdate_pa_kernel(
         regroup_points(0)
         mask_diagonal(2)
         sum_rows(2)
-        prepare(0)
+        clamp_sums(0)
         quantise_points(0)
+        invert_sums(0)
+        scale_rows(0)
+        transpose_edges(0)
+        clamp_sums(1)
         mask_diagonal(3)
-        prepare(1)
+        invert_sums(1)
+        scale_rows(1)
+        transpose_edges(1)
+        collect_transposed(0, 0)
+        collect_transposed(0, 1)
         for i in range(UNITS):
             quantise_edges(i)
+            if i >= 1:
+                quantise_x(i - 1)
             if i + 3 < UNITS:
                 sum_rows(i + 3)
             aggregate(i)
-            prepare(i + 2)
-            if i >= 1:
-                quantise_x(i - 1)
-            if i + 4 < UNITS:
-                mask_diagonal(i + 4)
             if i + 2 < UNITS and i % 2 == 0:
                 regroup_points(i // 2 + 1)
+            if i + 2 < UNITS:
+                clamp_sums(i + 2)
+            if i + 1 < UNITS:
+                collect_transposed(i + 1, 0)
+            if i + 2 < UNITS:
+                invert_sums(i + 2)
+            if i + 1 < UNITS:
+                collect_transposed(i + 1, 1)
+            if i + 4 < UNITS:
+                mask_diagonal(i + 4)
             if i + 1 < UNITS and i % 2 == 1:
                 quantise_points(i // 2 + 1)
+            if i + 2 < UNITS:
+                scale_rows(i + 2)
+            if i >= 2:
+                first = (i % 2) * (CHANNEL_TILES // 2)
+                survey(i // 2 - 1, range(first, first + CHANNEL_TILES // 2))
+            if i + 2 < UNITS:
+                transpose_edges(i + 2)
         quantise_x(UNITS - 1)
+
+        gain_shift_ps = psum.tile([P, P], BF16, tag="bank")
+        nc.tensor.transpose(gain_shift_ps[:], gain_shift_rows[:], ident_bf16[:])
+        gain_shift = const.tile([P, 2 * CHANNEL_TILES], F32)
+        nc.vector.tensor_copy(out=gain_shift[:], in_=gain_shift_ps[:, 0 : 2 * CHANNEL_TILES])
 
         z_banks = {}
         mean_var = {}
@@ -260,24 +293,12 @@ def tile_yuyipointupdate_pa_kernel(
         y_shift = {}
         y = {}
 
-        def convolve(ot):
-            channels = slice(ot * P, (ot + 1) * P)
-            stats = small.tile([P, GRAPHS, BN_STATS_DIM], F32)
-            for b in range(GRAPHS):
-                z_banks[ot, b] = psum.tile([P, NODES], F32, name="z_%d_%d" % (ot, b), tag="bank")
-                for g in range(K_GROUPS):
-                    nc.tensor.matmul_mx(
-                        out=z_banks[ot, b][:],
-                        lhsT=w_words[:, g, channels].bitcast(FP8X4),
-                        lhsT_scale=w_scales[:, g, channels],
-                        rhs=x_codes[2 * b + g][:].bitcast(FP8X4),
-                        rhs_scale=x_scales[2 * b + g][:],
-                        start=(g == 0),
-                        stop=(g == K_GROUPS - 1),
-                    )
-                nc.vector.bn_stats(out=stats[:, b, :], in_=z_banks[ot, b][:])
+        def convolve_all(ot):
+            for b in reversed(range(GRAPHS)):
+                z_banks[ot, b] = convolve(ot, b)
+            nc.vector.bn_stats(out=stats[:, ot, GRAPHS - 1, :], in_=z_banks[ot, GRAPHS - 1][:])
             mean_var[ot] = small.tile([P, 2], F32, name="mean_var_%d" % ot, tag="mean_var")
-            nc.vector.bn_aggr(out=mean_var[ot][:], in_=stats[:].rearrange("p b s -> p (b s)"))
+            nc.vector.bn_aggr(out=mean_var[ot][:], in_=stats[:, ot, :, :].rearrange("p b s -> p (b s)"))
 
         def affine(ot):
             variance_eps = small.tile([P, 1], F32)
@@ -316,11 +337,11 @@ def tile_yuyipointupdate_pa_kernel(
                     out=out[graphs, channels, :].rearrange("b p n -> p b n"), in_=y[ot][:, graphs, :]
                 )
 
-        convolve(0)
+        convolve_all(0)
         affine(0)
         for ot in range(CHANNEL_TILES):
             normalise(ot)
             if ot + 1 < CHANNEL_TILES:
-                convolve(ot + 1)
+                convolve_all(ot + 1)
                 affine(ot + 1)
             leaky_relu_and_store(ot)

@@ -55,8 +55,8 @@ def tile_yuyipointupdate_pa_kernel(
         nc.vector.tensor_scalar(
             out=off_diagonal[:], in0=ident_bf16[:], scalar1=-1.0, scalar2=1.0, op0=ALU.mult, op1=ALU.add
         )
-        minus_half = const.tile([P, 1], F32)
-        nc.vector.memset(minus_half[:], -0.5)
+        eps_bn = const.tile([P, 1], F32)
+        nc.vector.memset(eps_bn[:], EPS_BN)
         gain_shift_rows = const.tile([P, P], BF16)
         nc.vector.memset(gain_shift_rows[:], 0.0)
         w_scales = keep.tile([P, K_GROUPS, CHANNELS], U8, align_bytes=64)
@@ -103,11 +103,9 @@ def tile_yuyipointupdate_pa_kernel(
 
         def regroup_points(b):
             point_grouped[b] = work.tile([P, PACK, P, PACK], BF16, align_bytes=64, name="point_grouped_%d" % b, tag="point_grouped")
-            by_word = point_raw[b][:].rearrange("q t (pp tt) -> q tt pp t", tt=PACK)
-            if b == 0:
-                nc.vector.tensor_copy(out=point_grouped[b][:], in_=by_word)
-            else:
-                nc.scalar.copy(out=point_grouped[b][:], in_=by_word)
+            nc.vector.tensor_copy(
+                out=point_grouped[b][:], in_=point_raw[b][:].rearrange("q t (pp tt) -> q tt pp t", tt=PACK)
+            )
 
         def quantise_points(b):
             point_codes[b] = work.tile([P, FEATURES], U32, align_bytes=64, name="point_codes_%d" % b, tag="point_codes")
@@ -211,27 +209,18 @@ def tile_yuyipointupdate_pa_kernel(
                 in_=x_grouped[unit][:].rearrange("p n t -> p (n t)"),
             )
 
-        stats = keep.tile([P, CHANNEL_TILES, GRAPHS, BN_STATS_DIM], F32)
-
-        def convolve(ot, b):
-            channels = slice(ot * P, (ot + 1) * P)
-            z = psum.tile([P, NODES], F32, name="z_%d_%d" % (ot, b), tag="bank")
-            for g in range(K_GROUPS):
-                nc.tensor.matmul_mx(
-                    out=z[:],
-                    lhsT=w_words[:, g, channels].bitcast(FP8X4),
-                    lhsT_scale=w_scales[:, g, channels],
-                    rhs=x_codes[2 * b + g][:].bitcast(FP8X4),
-                    rhs_scale=x_scales[2 * b + g][:],
-                    start=(g == 0),
-                    stop=(g == K_GROUPS - 1),
-                )
-            return z
-
-        def survey(b, channel_tiles):
-            for ot in channel_tiles:
-                z = convolve(ot, b)
-                nc.vector.bn_stats(out=stats[:, ot, b, :], in_=z[:])
+        def prepare(unit):
+            if unit < UNITS:
+                clamp_sums(unit)
+            if 1 <= unit <= UNITS:
+                collect_transposed(unit - 1, 0)
+            if unit < UNITS:
+                invert_sums(unit)
+            if 1 <= unit <= UNITS:
+                collect_transposed(unit - 1, 1)
+            if unit < UNITS:
+                scale_rows(unit)
+                transpose_edges(unit)
 
         mask_diagonal(0)
         sum_rows(0)
@@ -240,108 +229,110 @@ def tile_yuyipointupdate_pa_kernel(
         regroup_points(0)
         mask_diagonal(2)
         sum_rows(2)
-        clamp_sums(0)
+        prepare(0)
         quantise_points(0)
-        invert_sums(0)
-        scale_rows(0)
-        transpose_edges(0)
-        clamp_sums(1)
         mask_diagonal(3)
-        invert_sums(1)
-        scale_rows(1)
-        transpose_edges(1)
-        collect_transposed(0, 0)
-        collect_transposed(0, 1)
+        prepare(1)
         for i in range(UNITS):
             quantise_edges(i)
-            if i >= 1:
-                quantise_x(i - 1)
             if i + 3 < UNITS:
                 sum_rows(i + 3)
             aggregate(i)
-            if i + 2 < UNITS and i % 2 == 0:
-                regroup_points(i // 2 + 1)
-            if i + 2 < UNITS:
-                clamp_sums(i + 2)
-            if i + 1 < UNITS:
-                collect_transposed(i + 1, 0)
-            if i + 2 < UNITS:
-                invert_sums(i + 2)
-            if i + 1 < UNITS:
-                collect_transposed(i + 1, 1)
+            prepare(i + 2)
+            if i >= 1:
+                quantise_x(i - 1)
             if i + 4 < UNITS:
                 mask_diagonal(i + 4)
+            if i + 2 < UNITS and i % 2 == 0:
+                regroup_points(i // 2 + 1)
             if i + 1 < UNITS and i % 2 == 1:
                 quantise_points(i // 2 + 1)
-            if i + 2 < UNITS:
-                scale_rows(i + 2)
-            if i >= 2:
-                first = (i % 2) * (CHANNEL_TILES // 2)
-                survey(i // 2 - 1, range(first, first + CHANNEL_TILES // 2))
-            if i + 2 < UNITS:
-                transpose_edges(i + 2)
-        quantise_x(UNITS - 1)
 
         gain_shift_ps = psum.tile([P, P], BF16, tag="bank")
         nc.tensor.transpose(gain_shift_ps[:], gain_shift_rows[:], ident_bf16[:])
-        gain_shift = const.tile([P, 2 * CHANNEL_TILES], F32)
-        nc.vector.tensor_copy(out=gain_shift[:], in_=gain_shift_ps[:, 0 : 2 * CHANNEL_TILES])
+        gain_pm = const.tile([P, CHANNEL_TILES, 2], F32)
+        nc.vector.tensor_copy(out=gain_pm[:, :, 0], in_=gain_shift_ps[:, 0:CHANNEL_TILES])
+        nc.vector.tensor_scalar_mul(out=gain_pm[:, :, 1], in0=gain_shift_ps[:, 0:CHANNEL_TILES], scalar1=-1.0)
+        shift = const.tile([P, CHANNEL_TILES], F32)
+        nc.vector.tensor_copy(out=shift[:], in_=gain_shift_ps[:, CHANNEL_TILES : 2 * CHANNEL_TILES])
 
         z_banks = {}
+        stats = {}
         mean_var = {}
         y_scale = {}
         y_shift = {}
         y = {}
+        negative_part = {}
 
-        def convolve_all(ot):
-            for b in reversed(range(GRAPHS)):
-                z_banks[ot, b] = convolve(ot, b)
-            nc.vector.bn_stats(out=stats[:, ot, GRAPHS - 1, :], in_=z_banks[ot, GRAPHS - 1][:])
-            mean_var[ot] = small.tile([P, 2], F32, name="mean_var_%d" % ot, tag="mean_var")
-            nc.vector.bn_aggr(out=mean_var[ot][:], in_=stats[:, ot, :, :].rearrange("p b s -> p (b s)"))
+        def convolve(ot, b):
+            channels = slice(ot * P, (ot + 1) * P)
+            if b == 0:
+                stats[ot] = small.tile([P, GRAPHS, BN_STATS_DIM], F32, name="stats_%d" % ot, tag="stats")
+            z_banks[ot, b] = psum.tile([P, NODES], F32, name="z_%d_%d" % (ot, b), tag="bank")
+            for g in range(K_GROUPS):
+                nc.tensor.matmul_mx(
+                    out=z_banks[ot, b][:],
+                    lhsT=w_words[:, g, channels].bitcast(FP8X4),
+                    lhsT_scale=w_scales[:, g, channels],
+                    rhs=x_codes[2 * b + g][:].bitcast(FP8X4),
+                    rhs_scale=x_scales[2 * b + g][:],
+                    start=(g == 0),
+                    stop=(g == K_GROUPS - 1),
+                )
+            nc.vector.bn_stats(out=stats[ot][:, b, :], in_=z_banks[ot, b][:])
 
         def affine(ot):
-            variance_eps = small.tile([P, 1], F32)
-            nc.gpsimd.tensor_scalar_add(out=variance_eps[:], in0=mean_var[ot][:, 1:2], scalar1=EPS_BN)
+            mean_var[ot] = small.tile([P, 2], F32, name="mean_var_%d" % ot, tag="mean_var")
+            nc.vector.bn_aggr(out=mean_var[ot][:], in_=stats[ot][:].rearrange("p b s -> p (b s)"))
             rstd = small.tile([P, 1], F32)
-            nc.gpsimd.tensor_tensor(out=rstd[:], in0=variance_eps[:], in1=minus_half[:], op=ALU.pow)
-            y_scale[ot] = small.tile([P, 1], F32, name="y_scale_%d" % ot, tag="y_scale")
-            nc.gpsimd.tensor_mul(out=y_scale[ot][:], in0=rstd[:], in1=gain_shift[:, ot : ot + 1])
-            mean_scaled = small.tile([P, 1], F32)
-            nc.gpsimd.tensor_mul(out=mean_scaled[:], in0=mean_var[ot][:, 0:1], in1=y_scale[ot][:])
+            nc.scalar.activation(out=rstd[:], in_=mean_var[ot][:, 1:2], func=ACT.Abs_reciprocal_sqrt, bias=eps_bn[:])
+            y_scale[ot] = small.tile([P, 2], F32, name="y_scale_%d" % ot, tag="y_scale")
+            nc.scalar.activation(out=y_scale[ot][:], in_=gain_pm[:, ot, :], func=ACT.Copy, scale=rstd[:])
             y_shift[ot] = small.tile([P, 1], F32, name="y_shift_%d" % ot, tag="y_shift")
-            nc.gpsimd.tensor_sub(
-                out=y_shift[ot][:], in0=gain_shift[:, CHANNEL_TILES + ot : CHANNEL_TILES + ot + 1], in1=mean_scaled[:]
+            nc.scalar.activation(
+                out=y_shift[ot][:],
+                in_=mean_var[ot][:, 0:1],
+                func=ACT.Identity,
+                scale=y_scale[ot][:, 1:2],
+                bias=shift[:, ot : ot + 1],
             )
 
         def normalise(ot):
             y[ot] = work.tile([P, GRAPHS, NODES], F32, name="y_%d" % ot, tag="y")
+            negative_part[ot] = work.tile([P, NODES], F32, name="negative_part_%d" % ot, tag="negative_part")
             for b in range(GRAPHS):
                 nc.scalar.activation(
                     out=y[ot][:, b, :],
                     in_=z_banks[ot, b][:],
                     func=ACT.Identity,
-                    scale=y_scale[ot][:],
+                    scale=y_scale[ot][:, 0:1],
                     bias=y_shift[ot][:],
                 )
+                if b == 1:
+                    nc.scalar.activation(
+                        out=negative_part[ot][:], in_=y[ot][:, 0, :], func=ACT.Relu, scale=NEG_SLOPE - 1.0
+                    )
 
         def leaky_relu_and_store(ot):
             channels = slice(ot * P, (ot + 1) * P)
-            for half in range(2):
-                graphs = slice(2 * half, 2 * half + 2)
-                y_half = y[ot][:, graphs, :].rearrange("p b n -> p (b n)")
+            nc.gpsimd.tensor_add(out=y[ot][:, 0, :], in0=y[ot][:, 0, :], in1=negative_part[ot][:])
+            for first, end in ((1, 2), (2, GRAPHS)):
+                y_part = y[ot][:, first:end, :].rearrange("p b n -> p (b n)")
                 nc.vector.scalar_tensor_tensor(
-                    out=y_half, in0=y_half, scalar=NEG_SLOPE, in1=y_half, op0=ALU.mult, op1=ALU.max
+                    out=y_part, in0=y_part, scalar=NEG_SLOPE, in1=y_part, op0=ALU.mult, op1=ALU.max
                 )
-                nc.sync.dma_start(
-                    out=out[graphs, channels, :].rearrange("b p n -> p b n"), in_=y[ot][:, graphs, :]
-                )
+                stored = slice(end - 2, end)
+                nc.sync.dma_start(out=out[stored, channels, :].rearrange("b p n -> p b n"), in_=y[ot][:, stored, :])
 
-        convolve_all(0)
+        for b in range(GRAPHS - 1):
+            convolve(0, b)
+        quantise_x(UNITS - 1)
+        convolve(0, GRAPHS - 1)
         affine(0)
         for ot in range(CHANNEL_TILES):
             normalise(ot)
             if ot + 1 < CHANNEL_TILES:
-                convolve_all(ot + 1)
+                for b in range(GRAPHS):
+                    convolve(ot + 1, b)
                 affine(ot + 1)
             leaky_relu_and_store(ot)

@@ -25,6 +25,9 @@ EPS_L1 = 1e-12
 EPS_BN = 1e-5
 NEG_SLOPE = 0.01
 BN_STATS_DIM = 6
+SIGN_CLEARED = 0x7FFF7FFF
+HEAD_UNITS = 2
+SCALAR_ROW_TILES = 1
 
 FLOPS = 2 * GRAPHS * (2 * NODES * NODES * FEATURES + CHANNELS * CHANNELS * NODES)
 
@@ -64,15 +67,22 @@ def tile_yuyipointupdate_pa_kernel(
 
         edge_sb = {}
         point_raw = {}
-        for b in range(GRAPHS):
-            for e in range(2):
-                edge_sb[2 * b + e] = inputs.tile([P, NODE_TILES, NODES], BF16, name="edge_%d" % (2 * b + e))
-                nc.sync.dma_start(out=edge_sb[2 * b + e][:], in_=edges[e][b].rearrange("(r p) m -> p r m", p=P))
+        def load_edges(unit):
+            edge_sb[unit] = inputs.tile([P, NODE_TILES, NODES], BF16, name="edge_%d" % unit)
+            nc.sync.dma_start(out=edge_sb[unit][:], in_=edges[unit % 2][unit // 2].rearrange("(r p) m -> p r m", p=P))
+
+        def load_points(b):
             point_raw[b] = inputs.tile([P, PACK, FEATURES], BF16, name="point_%d" % b)
             nc.sync.dma_start(
                 out=point_raw[b][:].rearrange("q (u e) d -> q u e d", u=2),
                 in_=point_node[b].rearrange("(u q e) d -> q u e d", u=2, e=2),
             )
+
+        for unit in range(UNITS):
+            load_edges(unit)
+            if unit >= 2 and unit % 2 == 0:
+                load_points(unit // 2 - 1)
+        load_points(GRAPHS - 1)
         nc.sync.dma_start(out=gain_shift_rows[0:CHANNEL_TILES, :], in_=g1.rearrange("(t p) -> t p", p=P))
         nc.sync.dma_start(
             out=gain_shift_rows[CHANNEL_TILES : 2 * CHANNEL_TILES, :], in_=b1.rearrange("(t p) -> t p", p=P)
@@ -91,6 +101,8 @@ def tile_yuyipointupdate_pa_kernel(
         point_grouped = {}
         row_sum = {}
         row_scale = {}
+        magnitude = {}
+        folded = {}
         transposed = {}
         edge_grouped = {}
         edge_codes = {}
@@ -127,9 +139,12 @@ def tile_yuyipointupdate_pa_kernel(
                 op=ALU.mult,
             )
 
+        def scalar_row_tiles(unit):
+            return NODE_TILES if unit < HEAD_UNITS else SCALAR_ROW_TILES
+
         def sum_rows(unit):
             row_sum[unit] = small.tile([P, NODE_TILES], F32, name="row_sum_%d" % unit, tag="row_sum")
-            for r in range(NODE_TILES):
+            for r in range(scalar_row_tiles(unit)):
                 magnitudes = work.tile([P, NODES], BF16)
                 nc.scalar.activation(
                     out=magnitudes[:],
@@ -137,6 +152,35 @@ def tile_yuyipointupdate_pa_kernel(
                     func=ACT.Abs,
                     accum_out=row_sum[unit][:, r : r + 1],
                 )
+
+        def take_magnitudes(unit):
+            first = scalar_row_tiles(unit)
+            magnitude[unit] = work.tile([P, NODE_TILES, NODES], BF16, name="magnitude_%d" % unit, tag="magnitude")
+            nc.vector.tensor_scalar(
+                out=magnitude[unit][:, first:, :].bitcast(I32),
+                in0=edge_sb[unit][:, first:, :].bitcast(I32),
+                scalar1=SIGN_CLEARED,
+                scalar2=None,
+                op0=ALU.bitwise_and,
+            )
+
+        def fold_rows(unit):
+            folded[unit] = psum.tile([P, NODE_TILES, P], F32, name="folded_%d" % unit, tag="bank")
+            for r in range(scalar_row_tiles(unit), NODE_TILES):
+                for c in range(NODE_TILES):
+                    nc.tensor.matmul(
+                        folded[unit][:, r, :],
+                        lhsT=ident_bf16[:],
+                        rhs=magnitude[unit][:, r, c * P : (c + 1) * P],
+                        start=(c == 0),
+                        stop=(c == NODE_TILES - 1),
+                    )
+
+        def reduce_folded(unit):
+            first = scalar_row_tiles(unit)
+            nc.vector.tensor_reduce(
+                out=row_sum[unit][:, first:], in_=folded[unit][:, first:, :], axis=mybir.AxisListType.X, op=ALU.add
+            )
 
         def clamp_sums(unit):
             nc.vector.tensor_scalar_max(out=row_sum[unit][:], in0=row_sum[unit][:], scalar1=EPS_L1)
@@ -167,7 +211,7 @@ def tile_yuyipointupdate_pa_kernel(
             if half == 0:
                 edge_grouped[unit] = work.tile([P, NODES, PACK], BF16, align_bytes=64, name="edge_grouped_%d" % unit, tag="edge_grouped")
             grouped_words = edge_grouped[unit][:].bitcast(F32)
-            nc.vector.tensor_copy(
+            nc.scalar.copy(
                 out=grouped_words[:, half * 2 * P : (half + 1) * 2 * P, :].rearrange("q (r n) u -> q r n u", r=2),
                 in_=transposed[unit, half][:].rearrange("q r u n -> q r n u"),
             )
@@ -209,44 +253,39 @@ def tile_yuyipointupdate_pa_kernel(
                 in_=x_grouped[unit][:].rearrange("p n t -> p (n t)"),
             )
 
-        def prepare(unit):
-            if unit < UNITS:
-                clamp_sums(unit)
-            if 1 <= unit <= UNITS:
-                collect_transposed(unit - 1, 0)
-            if unit < UNITS:
-                invert_sums(unit)
-            if 1 <= unit <= UNITS:
-                collect_transposed(unit - 1, 1)
-            if unit < UNITS:
-                scale_rows(unit)
-                transpose_edges(unit)
+        def exists(unit):
+            return 0 <= unit < UNITS
 
-        mask_diagonal(0)
-        sum_rows(0)
-        mask_diagonal(1)
-        sum_rows(1)
-        regroup_points(0)
-        mask_diagonal(2)
-        sum_rows(2)
-        prepare(0)
-        quantise_points(0)
-        mask_diagonal(3)
-        prepare(1)
-        for i in range(UNITS):
-            quantise_edges(i)
-            if i + 3 < UNITS:
-                sum_rows(i + 3)
-            aggregate(i)
-            prepare(i + 2)
-            if i >= 1:
-                quantise_x(i - 1)
-            if i + 4 < UNITS:
+        for i in range(-4, UNITS):
+            if exists(i):
+                quantise_edges(i)
+            if exists(i + 2):
+                clamp_sums(i + 2)
+            if exists(i + 4):
                 mask_diagonal(i + 4)
-            if i + 2 < UNITS and i % 2 == 0:
-                regroup_points(i // 2 + 1)
-            if i + 1 < UNITS and i % 2 == 1:
-                quantise_points(i // 2 + 1)
+            if exists(i + 2):
+                invert_sums(i + 2)
+            if exists(i + 3) and i + 3 >= HEAD_UNITS:
+                reduce_folded(i + 3)
+            if exists(i + 4):
+                sum_rows(i + 4)
+            if exists(i + 1):
+                collect_transposed(i + 1, 0)
+                collect_transposed(i + 1, 1)
+            if exists(i):
+                aggregate(i)
+            if exists(i + 2):
+                scale_rows(i + 2)
+                transpose_edges(i + 2)
+            if exists(i + 4) and i + 4 >= HEAD_UNITS:
+                take_magnitudes(i + 4)
+                fold_rows(i + 4)
+            if exists(i - 1):
+                quantise_x(i - 1)
+            if exists(i + 2) and i % 2 == 0:
+                regroup_points((i + 2) // 2)
+            if exists(i + 1) and i % 2 == 1:
+                quantise_points((i + 1) // 2)
 
         gain_shift_ps = psum.tile([P, P], BF16, tag="bank")
         nc.tensor.transpose(gain_shift_ps[:], gain_shift_rows[:], ident_bf16[:])

@@ -26,7 +26,8 @@ EPS_BN = 1e-5
 NEG_SLOPE = 0.01
 BN_STATS_DIM = 6
 SIGN_CLEARED = 0x7FFF7FFF
-HEAD_UNITS = 2
+HEAD_UNITS = 3
+SHARED_COLUMN = 2 * NODES + P
 SCALAR_ROW_TILES = 1
 
 FLOPS = 2 * GRAPHS * (2 * NODES * NODES * FEATURES + CHANNELS * CHANNELS * NODES)
@@ -50,6 +51,10 @@ def tile_yuyipointupdate_pa_kernel(
         psum = ctx.enter_context(tc.psum_pool(name="psum", bufs=8))
         ctx.enter_context(tc.manual_schedule())
 
+        eps_bn = const.tile([P, 1], F32)
+        nc.vector.memset(eps_bn[:], EPS_BN)
+        table_loader = const.tile([P, 1], F32)
+        nc.scalar.activation(out=table_loader[:], in_=eps_bn[:], func=ACT.Abs_reciprocal_sqrt)
         ident_f32 = const.tile([P, P], F32)
         make_identity(nc, ident_f32[:])
         ident_bf16 = const.tile([P, P], BF16)
@@ -58,8 +63,6 @@ def tile_yuyipointupdate_pa_kernel(
         nc.vector.tensor_scalar(
             out=off_diagonal[:], in0=ident_bf16[:], scalar1=-1.0, scalar2=1.0, op0=ALU.mult, op1=ALU.add
         )
-        eps_bn = const.tile([P, 1], F32)
-        nc.vector.memset(eps_bn[:], EPS_BN)
         gain_shift_rows = const.tile([P, P], BF16)
         nc.vector.memset(gain_shift_rows[:], 0.0)
         w_scales = keep.tile([P, K_GROUPS, CHANNELS], U8, align_bytes=64)
@@ -129,6 +132,7 @@ def tile_yuyipointupdate_pa_kernel(
             )
 
         def mask_diagonal(unit):
+            row_sum[unit] = small.tile([P, NODE_TILES], F32, name="row_sum_%d" % unit, tag="row_sum")
             diagonal_blocks = edge_sb[unit][:].rearrange("p r (c j) -> p (r c) j", j=P)[
                 :, 0 : NODE_TILES * NODE_TILES : NODE_TILES + 1, :
             ]
@@ -140,10 +144,11 @@ def tile_yuyipointupdate_pa_kernel(
             )
 
         def scalar_row_tiles(unit):
+            if unit == 0:
+                return 2
             return NODE_TILES if unit < HEAD_UNITS else SCALAR_ROW_TILES
 
         def sum_rows(unit):
-            row_sum[unit] = small.tile([P, NODE_TILES], F32, name="row_sum_%d" % unit, tag="row_sum")
             for r in range(scalar_row_tiles(unit)):
                 magnitudes = work.tile([P, NODES], BF16)
                 nc.scalar.activation(
@@ -152,6 +157,15 @@ def tile_yuyipointupdate_pa_kernel(
                     func=ACT.Abs,
                     accum_out=row_sum[unit][:, r : r + 1],
                 )
+
+        def sum_rows_on_vector(unit, first):
+            nc.vector.tensor_reduce(
+                out=row_sum[unit][:, first:],
+                in_=edge_sb[unit][:, first:, :],
+                axis=mybir.AxisListType.X,
+                op=ALU.add,
+                apply_absolute_value=True,
+            )
 
         def take_magnitudes(unit):
             first = scalar_row_tiles(unit)
@@ -230,7 +244,7 @@ def tile_yuyipointupdate_pa_kernel(
             x_grouped[unit] = work.tile([P, NODES, PACK], BF16, align_bytes=64, name="x_grouped_%d" % unit, tag="x_grouped")
             for j in range(NODE_TILES):
                 nodes = slice(j * P, (j + 1) * P)
-                aggregated = psum.tile([P, PACK, P], F32, tag="bank")
+                aggregated = psum.tile([P, PACK, P], F32, name="aggregated_%d_%d" % (unit, j), tag="bank")
                 for tt in range(PACK):
                     columns = slice(tt * P, (tt + 1) * P)
                     nc.tensor.matmul_mx(
@@ -253,51 +267,10 @@ def tile_yuyipointupdate_pa_kernel(
                 in_=x_grouped[unit][:].rearrange("p n t -> p (n t)"),
             )
 
-        def exists(unit):
-            return 0 <= unit < UNITS
-
-        for i in range(-4, UNITS):
-            if exists(i):
-                quantise_edges(i)
-            if exists(i + 2):
-                clamp_sums(i + 2)
-            if exists(i + 4):
-                mask_diagonal(i + 4)
-            if exists(i + 2):
-                invert_sums(i + 2)
-            if exists(i + 3) and i + 3 >= HEAD_UNITS:
-                reduce_folded(i + 3)
-            if exists(i + 4):
-                sum_rows(i + 4)
-            if exists(i + 1):
-                collect_transposed(i + 1, 0)
-                collect_transposed(i + 1, 1)
-            if exists(i):
-                aggregate(i)
-            if exists(i + 2):
-                scale_rows(i + 2)
-                transpose_edges(i + 2)
-            if exists(i + 4) and i + 4 >= HEAD_UNITS:
-                take_magnitudes(i + 4)
-                fold_rows(i + 4)
-            if exists(i - 1):
-                quantise_x(i - 1)
-            if exists(i + 2) and i % 2 == 0:
-                regroup_points((i + 2) // 2)
-            if exists(i + 1) and i % 2 == 1:
-                quantise_points((i + 1) // 2)
-
-        gain_shift_ps = psum.tile([P, P], BF16, tag="bank")
-        nc.tensor.transpose(gain_shift_ps[:], gain_shift_rows[:], ident_bf16[:])
-        gain_pm = const.tile([P, CHANNEL_TILES, 2], F32)
-        nc.vector.tensor_copy(out=gain_pm[:, :, 0], in_=gain_shift_ps[:, 0:CHANNEL_TILES])
-        nc.vector.tensor_scalar_mul(out=gain_pm[:, :, 1], in0=gain_shift_ps[:, 0:CHANNEL_TILES], scalar1=-1.0)
-        shift = const.tile([P, CHANNEL_TILES], F32)
-        nc.vector.tensor_copy(out=shift[:], in_=gain_shift_ps[:, CHANNEL_TILES : 2 * CHANNEL_TILES])
-
         z_banks = {}
         stats = {}
         mean_var = {}
+        rstd = {}
         y_scale = {}
         y_shift = {}
         y = {}
@@ -320,13 +293,19 @@ def tile_yuyipointupdate_pa_kernel(
                 )
             nc.vector.bn_stats(out=stats[ot][:, b, :], in_=z_banks[ot, b][:])
 
-        def affine(ot):
+        def aggregate_statistics(ot):
             mean_var[ot] = small.tile([P, 2], F32, name="mean_var_%d" % ot, tag="mean_var")
             nc.vector.bn_aggr(out=mean_var[ot][:], in_=stats[ot][:].rearrange("p b s -> p (b s)"))
-            rstd = small.tile([P, 1], F32)
-            nc.scalar.activation(out=rstd[:], in_=mean_var[ot][:, 1:2], func=ACT.Abs_reciprocal_sqrt, bias=eps_bn[:])
+
+        def invert_deviation(ot):
+            rstd[ot] = small.tile([P, 1], F32, name="rstd_%d" % ot, tag="rstd")
+            nc.scalar.activation(out=rstd[ot][:], in_=mean_var[ot][:, 1:2], func=ACT.Abs_reciprocal_sqrt, bias=eps_bn[:])
+
+        def make_scale(ot):
             y_scale[ot] = small.tile([P, 2], F32, name="y_scale_%d" % ot, tag="y_scale")
-            nc.scalar.activation(out=y_scale[ot][:], in_=gain_pm[:, ot, :], func=ACT.Copy, scale=rstd[:])
+            nc.scalar.activation(out=y_scale[ot][:], in_=gain_pm[:, ot, :], func=ACT.Copy, scale=rstd[ot][:])
+
+        def make_shift(ot):
             y_shift[ot] = small.tile([P, 1], F32, name="y_shift_%d" % ot, tag="y_shift")
             nc.scalar.activation(
                 out=y_shift[ot][:],
@@ -336,42 +315,171 @@ def tile_yuyipointupdate_pa_kernel(
                 bias=shift[:, ot : ot + 1],
             )
 
+        def apply_affine(ot, b):
+            nc.scalar.activation(
+                out=y[ot][:, b * NODES : (b + 1) * NODES],
+                in_=z_banks[ot, b][:],
+                func=ACT.Identity,
+                scale=y_scale[ot][:, 0:1],
+                bias=y_shift[ot][:],
+            )
+
+        def apply_affine_on_vector(ot, b):
+            nc.vector.tensor_scalar(
+                out=y[ot][:, b * NODES : (b + 1) * NODES],
+                in0=z_banks[ot, b][:],
+                scalar1=y_scale[ot][:, 0:1],
+                scalar2=y_shift[ot][:],
+                op0=ALU.mult,
+                op1=ALU.add,
+            )
+
+        def leaky_on_vector(ot, columns):
+            part = y[ot][:, columns]
+            nc.vector.scalar_tensor_tensor(
+                out=part, in0=part, scalar=NEG_SLOPE, in1=part, op0=ALU.mult, op1=ALU.max
+            )
+
+        def negate_part(ot, columns):
+            if ot not in negative_part:
+                negative_part[ot] = work.tile([P, GRAPHS * NODES], F32, name="negative_part_%d" % ot, tag="negative_part")
+            nc.scalar.activation(
+                out=negative_part[ot][:, columns],
+                in_=y[ot][:, columns],
+                func=ACT.Relu,
+                scale=NEG_SLOPE - 1.0,
+            )
+
+        def leaky_on_gpsimd(ot, columns):
+            part = y[ot][:, columns]
+            nc.gpsimd.tensor_add(out=part, in0=part, in1=negative_part[ot][:, columns])
+
+        def store(ot, first, end):
+            nc.sync.dma_start(
+                out=out[first:end, ot * P : (ot + 1) * P, :].rearrange("b p n -> p b n"),
+                in_=y[ot][:, first * NODES : end * NODES].rearrange("p (b n) -> p b n", n=NODES),
+            )
+
         def normalise(ot):
-            y[ot] = work.tile([P, GRAPHS, NODES], F32, name="y_%d" % ot, tag="y")
-            negative_part[ot] = work.tile([P, NODES], F32, name="negative_part_%d" % ot, tag="negative_part")
-            for b in range(GRAPHS):
-                nc.scalar.activation(
-                    out=y[ot][:, b, :],
-                    in_=z_banks[ot, b][:],
-                    func=ACT.Identity,
-                    scale=y_scale[ot][:, 0:1],
-                    bias=y_shift[ot][:],
-                )
-                if b == 1:
-                    nc.scalar.activation(
-                        out=negative_part[ot][:], in_=y[ot][:, 0, :], func=ACT.Relu, scale=NEG_SLOPE - 1.0
-                    )
+            y[ot] = work.tile([P, GRAPHS * NODES], F32, name="y_%d" % ot, tag="y")
+            for b in range(GRAPHS - 1):
+                apply_affine(ot, b)
+            negate_part(ot, slice(SHARED_COLUMN, 3 * NODES))
+            invert_deviation(ot + 1)
+            apply_affine(ot, 3)
+            make_scale(ot + 1)
+            negate_part(ot, slice(3 * NODES, 3 * NODES + 2 * P))
+            make_shift(ot + 1)
+            negate_part(ot, slice(3 * NODES + 2 * P, GRAPHS * NODES))
 
         def leaky_relu_and_store(ot):
-            channels = slice(ot * P, (ot + 1) * P)
-            nc.gpsimd.tensor_add(out=y[ot][:, 0, :], in0=y[ot][:, 0, :], in1=negative_part[ot][:])
-            for first, end in ((1, 2), (2, GRAPHS)):
-                y_part = y[ot][:, first:end, :].rearrange("p b n -> p (b n)")
-                nc.vector.scalar_tensor_tensor(
-                    out=y_part, in0=y_part, scalar=NEG_SLOPE, in1=y_part, op0=ALU.mult, op1=ALU.max
-                )
-                stored = slice(end - 2, end)
-                nc.sync.dma_start(out=out[stored, channels, :].rearrange("b p n -> p b n"), in_=y[ot][:, stored, :])
+            leaky_on_vector(ot, slice(0, SHARED_COLUMN))
+            store(ot, 0, 2)
+            leaky_on_gpsimd(ot, slice(SHARED_COLUMN, GRAPHS * NODES))
+            store(ot, 2, GRAPHS)
 
-        for b in range(GRAPHS - 1):
-            convolve(0, b)
-        quantise_x(UNITS - 1)
-        convolve(0, GRAPHS - 1)
-        affine(0)
+        def normalise_plainly(ot):
+            y[ot] = work.tile([P, GRAPHS * NODES], F32, name="y_%d" % ot, tag="y")
+            for b in range(GRAPHS):
+                apply_affine(ot, b)
+            if ot + 1 < CHANNEL_TILES:
+                invert_deviation(ot + 1)
+                make_scale(ot + 1)
+                make_shift(ot + 1)
+
+        def finish(ot):
+            for first, end in (((0, 2), (2, 4)) if ot + 1 < CHANNEL_TILES else ((0, 2), (2, 3), (3, 4))):
+                leaky_on_vector(ot, slice(first * NODES, end * NODES))
+                store(ot, first, end)
+
+        def exists(unit):
+            return 0 <= unit < UNITS
+
+        def folds(unit):
+            return exists(unit) and unit > 0 and scalar_row_tiles(unit) < NODE_TILES
+
+        mask_diagonal(0)
+        sum_rows(0)
+        sum_rows_on_vector(0, scalar_row_tiles(0))
+        mask_diagonal(1)
+        sum_rows(1)
+        clamp_sums(0)
+        mask_diagonal(2)
+        invert_sums(0)
+        scale_rows(0)
+        transpose_edges(0)
+        regroup_points(0)
+        collect_transposed(0, 0)
+        collect_transposed(0, 1)
+        sum_rows(2)
+        clamp_sums(1)
+        mask_diagonal(3)
+        invert_sums(1)
+        scale_rows(1)
+        transpose_edges(1)
+        if folds(3):
+            take_magnitudes(3)
+            fold_rows(3)
+        quantise_points(0)
+        for i in range(UNITS - 1):
+            quantise_edges(i)
+            if exists(i + 2):
+                clamp_sums(i + 2)
+            if exists(i + 4):
+                mask_diagonal(i + 4)
+            if exists(i + 2):
+                invert_sums(i + 2)
+            if folds(i + 3):
+                reduce_folded(i + 3)
+            if exists(i + 3):
+                sum_rows(i + 3)
+            if exists(i + 1):
+                collect_transposed(i + 1, 0)
+                collect_transposed(i + 1, 1)
+            aggregate(i)
+            if exists(i + 2):
+                scale_rows(i + 2)
+                transpose_edges(i + 2)
+            if folds(i + 4):
+                take_magnitudes(i + 4)
+                fold_rows(i + 4)
+            if exists(i - 1):
+                quantise_x(i - 1)
+            if exists(i + 2) and i % 2 == 0:
+                regroup_points((i + 2) // 2)
+            if exists(i + 1) and i % 2 == 1:
+                quantise_points((i + 1) // 2)
+
+        gain_shift_ps = psum.tile([P, P], BF16, tag="bank")
+        nc.tensor.transpose(gain_shift_ps[:], gain_shift_rows[:], ident_bf16[:])
+        gain_pm = const.tile([P, CHANNEL_TILES, 2], F32)
+        nc.vector.tensor_copy(out=gain_pm[:, :, 0], in_=gain_shift_ps[:, 0:CHANNEL_TILES])
+        nc.vector.tensor_scalar_mul(out=gain_pm[:, :, 1], in0=gain_shift_ps[:, 0:CHANNEL_TILES], scalar1=-1.0)
+        shift = const.tile([P, CHANNEL_TILES], F32)
+        nc.vector.tensor_copy(out=shift[:], in_=gain_shift_ps[:, CHANNEL_TILES : 2 * CHANNEL_TILES])
+
+        last = UNITS - 1
+        quantise_edges(last)
+        convolve(0, 0)
+        convolve(0, 1)
+        aggregate(last)
+        quantise_x(last - 1)
+        convolve(0, 2)
+        quantise_x(last)
+        convolve(0, 3)
+        aggregate_statistics(0)
+        invert_deviation(0)
+        make_scale(0)
+        make_shift(0)
+
         for ot in range(CHANNEL_TILES):
-            normalise(ot)
             if ot + 1 < CHANNEL_TILES:
                 for b in range(GRAPHS):
                     convolve(ot + 1, b)
-                affine(ot + 1)
-            leaky_relu_and_store(ot)
+                aggregate_statistics(ot + 1)
+            if ot + 2 < CHANNEL_TILES:
+                normalise(ot)
+                leaky_relu_and_store(ot)
+            else:
+                normalise_plainly(ot)
+                finish(ot)

@@ -27,7 +27,9 @@ NEG_SLOPE = 0.01
 BN_STATS_DIM = 6
 SIGN_CLEARED = 0x7FFF7FFF
 HEAD_UNITS = 3
-SHARED_COLUMN = 2 * NODES + P
+FOLD = 64
+FIRST_COLUMNS = 256
+SHARED_COLUMN = 1280
 SCALAR_ROW_TILES = 1
 
 FLOPS = 2 * GRAPHS * (2 * NODES * NODES * FEATURES + CHANNELS * CHANNELS * NODES)
@@ -47,12 +49,16 @@ def tile_yuyipointupdate_pa_kernel(
         inputs = ctx.enter_context(tc.tile_pool(name="inputs", bufs=1))
         keep = ctx.enter_context(tc.tile_pool(name="keep", bufs=1))
         work = ctx.enter_context(tc.tile_pool(name="work", bufs=3))
+        outputs = ctx.enter_context(tc.tile_pool(name="outputs", bufs=4))
         small = ctx.enter_context(tc.tile_pool(name="small", bufs=4))
-        psum = ctx.enter_context(tc.psum_pool(name="psum", bufs=8))
+        psum = ctx.enter_context(tc.psum_pool(name="psum", bufs=6))
+        early = ctx.enter_context(tc.psum_pool(name="early", bufs=2))
         ctx.enter_context(tc.manual_schedule())
 
         eps_bn = const.tile([P, 1], F32)
         nc.vector.memset(eps_bn[:], EPS_BN)
+        gain_shift_rows = const.tile([P, P], BF16)
+        nc.vector.memset(gain_shift_rows[:], 0.0)
         table_loader = const.tile([P, 1], F32)
         nc.scalar.activation(out=table_loader[:], in_=eps_bn[:], func=ACT.Abs_reciprocal_sqrt)
         ident_f32 = const.tile([P, P], F32)
@@ -63,16 +69,21 @@ def tile_yuyipointupdate_pa_kernel(
         nc.vector.tensor_scalar(
             out=off_diagonal[:], in0=ident_bf16[:], scalar1=-1.0, scalar2=1.0, op0=ALU.mult, op1=ALU.add
         )
-        gain_shift_rows = const.tile([P, P], BF16)
-        nc.vector.memset(gain_shift_rows[:], 0.0)
         w_scales = keep.tile([P, K_GROUPS, CHANNELS], U8, align_bytes=64)
         nc.vector.memset(w_scales[:].rearrange("p g n -> p (g n)").bitcast(I32), 0)
 
+        nc.scalar.dma_start(out=gain_shift_rows[0:CHANNEL_TILES, :], in_=g1.rearrange("(t p) -> t p", p=P))
+        nc.scalar.dma_start(
+            out=gain_shift_rows[CHANNEL_TILES : 2 * CHANNEL_TILES, :], in_=b1.rearrange("(t p) -> t p", p=P)
+        )
         edge_sb = {}
         point_raw = {}
         def load_edges(unit):
             edge_sb[unit] = inputs.tile([P, NODE_TILES, NODES], BF16, name="edge_%d" % unit)
-            nc.sync.dma_start(out=edge_sb[unit][:], in_=edges[unit % 2][unit // 2].rearrange("(r p) m -> p r m", p=P))
+            rows = edges[unit % 2][unit // 2].rearrange("(r p) m -> p r m", p=P)
+            step = NODE_TILES // 2 if unit == 0 else NODE_TILES
+            for r in range(0, NODE_TILES, step):
+                nc.sync.dma_start(out=edge_sb[unit][:, r : r + step, :], in_=rows[:, r : r + step, :])
 
         def load_points(b):
             point_raw[b] = inputs.tile([P, PACK, FEATURES], BF16, name="point_%d" % b)
@@ -83,13 +94,8 @@ def tile_yuyipointupdate_pa_kernel(
 
         for unit in range(UNITS):
             load_edges(unit)
-            if unit >= 2 and unit % 2 == 0:
-                load_points(unit // 2 - 1)
-        load_points(GRAPHS - 1)
-        nc.sync.dma_start(out=gain_shift_rows[0:CHANNEL_TILES, :], in_=g1.rearrange("(t p) -> t p", p=P))
-        nc.sync.dma_start(
-            out=gain_shift_rows[CHANNEL_TILES : 2 * CHANNEL_TILES, :], in_=b1.rearrange("(t p) -> t p", p=P)
-        )
+            if unit % 2 == 1:
+                load_points(unit // 2)
         w_words = keep.tile([P, K_GROUPS, CHANNELS], U32, align_bytes=64)
         for g in range(K_GROUPS):
             nc.sync.dma_start(
@@ -131,25 +137,21 @@ def tile_yuyipointupdate_pa_kernel(
                 in_=point_grouped[b][:].rearrange("q tt pp t -> q (tt pp t)"),
             )
 
-        def mask_diagonal(unit):
-            row_sum[unit] = small.tile([P, NODE_TILES], F32, name="row_sum_%d" % unit, tag="row_sum")
+        def mask_diagonal(unit, first=0, end=NODE_TILES):
+            if first == 0:
+                row_sum[unit] = small.tile([P, NODE_TILES], F32, name="row_sum_%d" % unit, tag="row_sum")
             diagonal_blocks = edge_sb[unit][:].rearrange("p r (c j) -> p (r c) j", j=P)[
-                :, 0 : NODE_TILES * NODE_TILES : NODE_TILES + 1, :
+                :, first * (NODE_TILES + 1) : (end - 1) * (NODE_TILES + 1) + 1 : NODE_TILES + 1, :
             ]
             nc.vector.tensor_tensor(
                 out=diagonal_blocks,
                 in0=diagonal_blocks,
-                in1=off_diagonal[:].unsqueeze(1).to_broadcast([P, NODE_TILES, P]),
+                in1=off_diagonal[:].unsqueeze(1).to_broadcast([P, end - first, P]),
                 op=ALU.mult,
             )
 
-        def scalar_row_tiles(unit):
-            if unit == 0:
-                return 2
-            return NODE_TILES if unit < HEAD_UNITS else SCALAR_ROW_TILES
-
-        def sum_rows(unit):
-            for r in range(scalar_row_tiles(unit)):
+        def sum_rows(unit, first=0, end=NODE_TILES):
+            for r in range(first, end):
                 magnitudes = work.tile([P, NODES], BF16)
                 nc.scalar.activation(
                     out=magnitudes[:],
@@ -158,42 +160,43 @@ def tile_yuyipointupdate_pa_kernel(
                     accum_out=row_sum[unit][:, r : r + 1],
                 )
 
-        def sum_rows_on_vector(unit, first):
+        def sum_rows_on_vector(unit, first, end):
             nc.vector.tensor_reduce(
-                out=row_sum[unit][:, first:],
-                in_=edge_sb[unit][:, first:, :],
+                out=row_sum[unit][:, first:end],
+                in_=edge_sb[unit][:, first:end, :],
                 axis=mybir.AxisListType.X,
                 op=ALU.add,
                 apply_absolute_value=True,
             )
 
         def take_magnitudes(unit):
-            first = scalar_row_tiles(unit)
             magnitude[unit] = work.tile([P, NODE_TILES, NODES], BF16, name="magnitude_%d" % unit, tag="magnitude")
             nc.vector.tensor_scalar(
-                out=magnitude[unit][:, first:, :].bitcast(I32),
-                in0=edge_sb[unit][:, first:, :].bitcast(I32),
+                out=magnitude[unit][:, SCALAR_ROW_TILES:, :].bitcast(I32),
+                in0=edge_sb[unit][:, SCALAR_ROW_TILES:, :].bitcast(I32),
                 scalar1=SIGN_CLEARED,
                 scalar2=None,
                 op0=ALU.bitwise_and,
             )
 
         def fold_rows(unit):
-            folded[unit] = psum.tile([P, NODE_TILES, P], F32, name="folded_%d" % unit, tag="bank")
-            for r in range(scalar_row_tiles(unit), NODE_TILES):
-                for c in range(NODE_TILES):
+            folded[unit] = psum.tile([P, NODE_TILES, FOLD], F32, name="folded_%d" % unit, tag="bank")
+            for r in range(SCALAR_ROW_TILES, NODE_TILES):
+                for c in range(0, NODES, FOLD):
                     nc.tensor.matmul(
                         folded[unit][:, r, :],
                         lhsT=ident_bf16[:],
-                        rhs=magnitude[unit][:, r, c * P : (c + 1) * P],
+                        rhs=magnitude[unit][:, r, c : c + FOLD],
                         start=(c == 0),
-                        stop=(c == NODE_TILES - 1),
+                        stop=(c + FOLD == NODES),
                     )
 
         def reduce_folded(unit):
-            first = scalar_row_tiles(unit)
             nc.vector.tensor_reduce(
-                out=row_sum[unit][:, first:], in_=folded[unit][:, first:, :], axis=mybir.AxisListType.X, op=ALU.add
+                out=row_sum[unit][:, SCALAR_ROW_TILES:],
+                in_=folded[unit][:, SCALAR_ROW_TILES:, :],
+                axis=mybir.AxisListType.X,
+                op=ALU.add,
             )
 
         def clamp_sums(unit):
@@ -239,12 +242,21 @@ def tile_yuyipointupdate_pa_kernel(
                 in_=edge_grouped[unit][:].rearrange("q n t -> q (n t)"),
             )
 
-        def aggregate(unit):
-            b = unit // 2
+        x_banks = {}
+
+        def take_x_banks(unit):
             x_grouped[unit] = work.tile([P, NODES, PACK], BF16, align_bytes=64, name="x_grouped_%d" % unit, tag="x_grouped")
+            x_banks[unit] = [
+                psum.tile([P, PACK, P], F32, name="aggregated_%d_%d" % (unit, j), tag="bank") for j in range(NODE_TILES)
+            ]
+
+        def aggregate(unit, scalar_tiles=NODE_TILES):
+            b = unit // 2
+            if unit not in x_banks:
+                take_x_banks(unit)
             for j in range(NODE_TILES):
                 nodes = slice(j * P, (j + 1) * P)
-                aggregated = psum.tile([P, PACK, P], F32, name="aggregated_%d_%d" % (unit, j), tag="bank")
+                aggregated = x_banks[unit][j]
                 for tt in range(PACK):
                     columns = slice(tt * P, (tt + 1) * P)
                     nc.tensor.matmul_mx(
@@ -256,7 +268,13 @@ def tile_yuyipointupdate_pa_kernel(
                         start=True,
                         stop=True,
                     )
-                nc.scalar.copy(out=x_grouped[unit][:, nodes, :], in_=aggregated[:].rearrange("p t n -> p n t"))
+                if j < scalar_tiles:
+                    nc.scalar.copy(out=x_grouped[unit][:, nodes, :], in_=aggregated[:].rearrange("p t n -> p n t"))
+
+        def copy_x_on_vector(unit, j):
+            nc.vector.tensor_copy(
+                out=x_grouped[unit][:, j * P : (j + 1) * P, :], in_=x_banks[unit][j][:].rearrange("p t n -> p n t")
+            )
 
         def quantise_x(unit):
             x_codes[unit] = keep.tile([P, NODES], U32, align_bytes=64, name="x_codes_%d" % unit)
@@ -280,7 +298,8 @@ def tile_yuyipointupdate_pa_kernel(
             channels = slice(ot * P, (ot + 1) * P)
             if b == 0:
                 stats[ot] = small.tile([P, GRAPHS, BN_STATS_DIM], F32, name="stats_%d" % ot, tag="stats")
-            z_banks[ot, b] = psum.tile([P, NODES], F32, name="z_%d_%d" % (ot, b), tag="bank")
+            pool, tag = (early, "early_bank") if ot % 2 == 0 and b < 2 else (psum, "bank")
+            z_banks[ot, b] = pool.tile([P, NODES], F32, name="z_%d_%d" % (ot, b), tag=tag)
             for g in range(K_GROUPS):
                 nc.tensor.matmul_mx(
                     out=z_banks[ot, b][:],
@@ -291,6 +310,8 @@ def tile_yuyipointupdate_pa_kernel(
                     start=(g == 0),
                     stop=(g == K_GROUPS - 1),
                 )
+
+        def take_statistics(ot, b):
             nc.vector.bn_stats(out=stats[ot][:, b, :], in_=z_banks[ot, b][:])
 
         def aggregate_statistics(ot):
@@ -316,6 +337,8 @@ def tile_yuyipointupdate_pa_kernel(
             )
 
         def apply_affine(ot, b):
+            if b == 0:
+                y[ot] = outputs.tile([P, GRAPHS * NODES], F32, name="y_%d" % ot, tag="y")
             nc.scalar.activation(
                 out=y[ot][:, b * NODES : (b + 1) * NODES],
                 in_=z_banks[ot, b][:],
@@ -342,7 +365,7 @@ def tile_yuyipointupdate_pa_kernel(
 
         def negate_part(ot, columns):
             if ot not in negative_part:
-                negative_part[ot] = work.tile([P, GRAPHS * NODES], F32, name="negative_part_%d" % ot, tag="negative_part")
+                negative_part[ot] = outputs.tile([P, GRAPHS * NODES], F32, name="negative_part_%d" % ot, tag="negative_part")
             nc.scalar.activation(
                 out=negative_part[ot][:, columns],
                 in_=y[ot][:, columns],
@@ -360,96 +383,40 @@ def tile_yuyipointupdate_pa_kernel(
                 in_=y[ot][:, first * NODES : end * NODES].rearrange("p (b n) -> p b n", n=NODES),
             )
 
-        def normalise(ot):
-            y[ot] = work.tile([P, GRAPHS * NODES], F32, name="y_%d" % ot, tag="y")
-            for b in range(GRAPHS - 1):
-                apply_affine(ot, b)
-            negate_part(ot, slice(SHARED_COLUMN, 3 * NODES))
+        def finish_shared(ot):
+            leaky_on_vector(ot, slice(0, FIRST_COLUMNS))
+            aggregate_statistics(ot + 1)
             invert_deviation(ot + 1)
-            apply_affine(ot, 3)
+            negate_part(ot, slice(SHARED_COLUMN, 3 * NODES))
             make_scale(ot + 1)
             negate_part(ot, slice(3 * NODES, 3 * NODES + 2 * P))
             make_shift(ot + 1)
             negate_part(ot, slice(3 * NODES + 2 * P, GRAPHS * NODES))
-
-        def leaky_relu_and_store(ot):
-            leaky_on_vector(ot, slice(0, SHARED_COLUMN))
+            leaky_on_vector(ot, slice(FIRST_COLUMNS, SHARED_COLUMN))
             store(ot, 0, 2)
             leaky_on_gpsimd(ot, slice(SHARED_COLUMN, GRAPHS * NODES))
             store(ot, 2, GRAPHS)
 
-        def normalise_plainly(ot):
-            y[ot] = work.tile([P, GRAPHS * NODES], F32, name="y_%d" % ot, tag="y")
+        def finish_alone(ot):
             for b in range(GRAPHS):
-                apply_affine(ot, b)
-            if ot + 1 < CHANNEL_TILES:
-                invert_deviation(ot + 1)
-                make_scale(ot + 1)
-                make_shift(ot + 1)
-
-        def finish(ot):
-            for first, end in (((0, 2), (2, 4)) if ot + 1 < CHANNEL_TILES else ((0, 2), (2, 3), (3, 4))):
-                leaky_on_vector(ot, slice(first * NODES, end * NODES))
-                store(ot, first, end)
+                leaky_on_vector(ot, slice(b * NODES, (b + 1) * NODES))
+                store(ot, b, b + 1)
 
         def exists(unit):
             return 0 <= unit < UNITS
 
         def folds(unit):
-            return exists(unit) and unit > 0 and scalar_row_tiles(unit) < NODE_TILES
+            return HEAD_UNITS <= unit < UNITS
 
-        mask_diagonal(0)
-        sum_rows(0)
-        sum_rows_on_vector(0, scalar_row_tiles(0))
+        mask_diagonal(0, 0, 2)
+        sum_rows(0, 0, 1)
+        sum_rows_on_vector(0, 1, 2)
+        mask_diagonal(0, 2, 4)
+        sum_rows(0, 2, 3)
+        sum_rows_on_vector(0, 3, 4)
         mask_diagonal(1)
-        sum_rows(1)
+        sum_rows(1, 0, 3)
         clamp_sums(0)
-        mask_diagonal(2)
-        invert_sums(0)
-        scale_rows(0)
-        transpose_edges(0)
-        regroup_points(0)
-        collect_transposed(0, 0)
-        collect_transposed(0, 1)
-        sum_rows(2)
-        clamp_sums(1)
-        mask_diagonal(3)
-        invert_sums(1)
-        scale_rows(1)
-        transpose_edges(1)
-        if folds(3):
-            take_magnitudes(3)
-            fold_rows(3)
-        quantise_points(0)
-        for i in range(UNITS - 1):
-            quantise_edges(i)
-            if exists(i + 2):
-                clamp_sums(i + 2)
-            if exists(i + 4):
-                mask_diagonal(i + 4)
-            if exists(i + 2):
-                invert_sums(i + 2)
-            if folds(i + 3):
-                reduce_folded(i + 3)
-            if exists(i + 3):
-                sum_rows(i + 3)
-            if exists(i + 1):
-                collect_transposed(i + 1, 0)
-                collect_transposed(i + 1, 1)
-            aggregate(i)
-            if exists(i + 2):
-                scale_rows(i + 2)
-                transpose_edges(i + 2)
-            if folds(i + 4):
-                take_magnitudes(i + 4)
-                fold_rows(i + 4)
-            if exists(i - 1):
-                quantise_x(i - 1)
-            if exists(i + 2) and i % 2 == 0:
-                regroup_points((i + 2) // 2)
-            if exists(i + 1) and i % 2 == 1:
-                quantise_points((i + 1) // 2)
-
         gain_shift_ps = psum.tile([P, P], BF16, tag="bank")
         nc.tensor.transpose(gain_shift_ps[:], gain_shift_rows[:], ident_bf16[:])
         gain_pm = const.tile([P, CHANNEL_TILES, 2], F32)
@@ -457,29 +424,89 @@ def tile_yuyipointupdate_pa_kernel(
         nc.vector.tensor_scalar_mul(out=gain_pm[:, :, 1], in0=gain_shift_ps[:, 0:CHANNEL_TILES], scalar1=-1.0)
         shift = const.tile([P, CHANNEL_TILES], F32)
         nc.vector.tensor_copy(out=shift[:], in_=gain_shift_ps[:, CHANNEL_TILES : 2 * CHANNEL_TILES])
+        sum_rows_on_vector(1, 3, 4)
+        invert_sums(0)
+        scale_rows(0)
+        transpose_edges(0)
+        regroup_points(0)
+        mask_diagonal(2)
+        clamp_sums(1)
+        quantise_points(0)
+        invert_sums(1)
+        mask_diagonal(3)
+        scale_rows(1)
+        transpose_edges(1)
+        collect_transposed(0, 0)
+        collect_transposed(0, 1)
+        sum_rows(2)
+        take_magnitudes(3)
+        fold_rows(3)
+        for i in range(UNITS - 1):
+            quantise_edges(i)
+            if exists(i + 2):
+                clamp_sums(i + 2)
+            if exists(i + 4):
+                mask_diagonal(i + 4)
+            if i == UNITS - 2:
+                take_statistics(0, 0)
+            if exists(i - 1) and not exists(i + 4):
+                quantise_x(i - 1)
+            if exists(i + 2):
+                invert_sums(i + 2)
+            if folds(i + 3):
+                reduce_folded(i + 3)
+                sum_rows(i + 3, 0, SCALAR_ROW_TILES)
+            if exists(i + 1):
+                collect_transposed(i + 1, 0)
+                collect_transposed(i + 1, 1)
+            aggregate(i, NODE_TILES - (1 if i == UNITS - 2 else 0))
+            if i % 2 == 1:
+                quantise_points((i + 1) // 2)
+            if exists(i + 2):
+                scale_rows(i + 2)
+                transpose_edges(i + 2)
+            if folds(i + 4):
+                take_magnitudes(i + 4)
+                fold_rows(i + 4)
+            if i == 4:
+                convolve(0, 0)
+            if i == 5:
+                convolve(0, 1)
+            if exists(i - 1) and exists(i + 4):
+                quantise_x(i - 1)
+            if i % 2 == 0 and exists(i + 2):
+                regroup_points((i + 2) // 2)
 
         last = UNITS - 1
         quantise_edges(last)
-        convolve(0, 0)
-        convolve(0, 1)
-        aggregate(last)
+        take_statistics(0, 1)
+        aggregate(last, NODE_TILES - 1)
+        copy_x_on_vector(last - 1, 3)
         quantise_x(last - 1)
         convolve(0, 2)
+        copy_x_on_vector(last, 3)
+        take_statistics(0, 2)
         quantise_x(last)
         convolve(0, 3)
+        take_statistics(0, 3)
         aggregate_statistics(0)
         invert_deviation(0)
         make_scale(0)
         make_shift(0)
 
         for ot in range(CHANNEL_TILES):
+            for b in range(GRAPHS):
+                apply_affine(ot, b)
             if ot + 1 < CHANNEL_TILES:
                 for b in range(GRAPHS):
                     convolve(ot + 1, b)
-                aggregate_statistics(ot + 1)
+                    take_statistics(ot + 1, b)
             if ot + 2 < CHANNEL_TILES:
-                normalise(ot)
-                leaky_relu_and_store(ot)
+                finish_shared(ot)
             else:
-                normalise_plainly(ot)
-                finish(ot)
+                if ot + 1 < CHANNEL_TILES:
+                    aggregate_statistics(ot + 1)
+                    invert_deviation(ot + 1)
+                    make_scale(ot + 1)
+                    make_shift(ot + 1)
+                finish_alone(ot)

@@ -29,7 +29,7 @@ SIGN_CLEARED = 0x7FFF7FFF
 HEAD_UNITS = 3
 FOLD = 64
 FIRST_COLUMNS = 256
-SHARED_COLUMN = 1280
+SHARED_COLUMN = 1216
 SCALAR_ROW_TILES = 1
 
 FLOPS = 2 * GRAPHS * (2 * NODES * NODES * FEATURES + CHANNELS * CHANNELS * NODES)
@@ -59,6 +59,8 @@ def tile_yuyipointupdate_pa_kernel(
         nc.vector.memset(eps_bn[:], EPS_BN)
         gain_shift_rows = const.tile([P, P], BF16)
         nc.vector.memset(gain_shift_rows[:], 0.0)
+        gain_pm = const.tile([P, CHANNEL_TILES, 2], F32)
+        shift = const.tile([P, CHANNEL_TILES], F32)
         table_loader = const.tile([P, 1], F32)
         nc.scalar.activation(out=table_loader[:], in_=eps_bn[:], func=ACT.Abs_reciprocal_sqrt)
         ident_f32 = const.tile([P, P], F32)
@@ -72,10 +74,6 @@ def tile_yuyipointupdate_pa_kernel(
         w_scales = keep.tile([P, K_GROUPS, CHANNELS], U8, align_bytes=64)
         nc.vector.memset(w_scales[:].rearrange("p g n -> p (g n)").bitcast(I32), 0)
 
-        nc.scalar.dma_start(out=gain_shift_rows[0:CHANNEL_TILES, :], in_=g1.rearrange("(t p) -> t p", p=P))
-        nc.scalar.dma_start(
-            out=gain_shift_rows[CHANNEL_TILES : 2 * CHANNEL_TILES, :], in_=b1.rearrange("(t p) -> t p", p=P)
-        )
         edge_sb = {}
         point_raw = {}
         def load_edges(unit):
@@ -94,8 +92,14 @@ def tile_yuyipointupdate_pa_kernel(
 
         for unit in range(UNITS):
             load_edges(unit)
-            if unit % 2 == 1:
-                load_points(unit // 2)
+            if unit == 1 or unit >= 4 and unit % 2 == 0:
+                load_points(max(0, unit // 2 - 1))
+            if unit == 3:
+                nc.sync.dma_start(out=gain_shift_rows[0:CHANNEL_TILES, :], in_=g1.rearrange("(t p) -> t p", p=P))
+                nc.sync.dma_start(
+                    out=gain_shift_rows[CHANNEL_TILES : 2 * CHANNEL_TILES, :], in_=b1.rearrange("(t p) -> t p", p=P)
+                )
+        load_points(GRAPHS - 1)
         w_words = keep.tile([P, K_GROUPS, CHANNELS], U32, align_bytes=64)
         for g in range(K_GROUPS):
             nc.sync.dma_start(
@@ -200,7 +204,7 @@ def tile_yuyipointupdate_pa_kernel(
             )
 
         def clamp_sums(unit):
-            nc.vector.tensor_scalar_max(out=row_sum[unit][:], in0=row_sum[unit][:], scalar1=EPS_L1)
+            nc.gpsimd.tensor_scalar_max(out=row_sum[unit][:], in0=row_sum[unit][:], scalar1=EPS_L1)
 
         def invert_sums(unit):
             row_scale[unit] = small.tile([P, NODE_TILES], F32, name="row_scale_%d" % unit, tag="row_scale")
@@ -276,63 +280,71 @@ def tile_yuyipointupdate_pa_kernel(
                 out=x_grouped[unit][:, j * P : (j + 1) * P, :], in_=x_banks[unit][j][:].rearrange("p t n -> p n t")
             )
 
-        def quantise_x(unit):
+        def quantise_x(unit, first=0, end=NODES):
+            if first == 0:
+                open_x_codes(unit)
+            nc.vector.quantize_mx(
+                out=x_codes[unit][:, first:end].bitcast(FP8X4),
+                scales=x_scales[unit][:, first:end],
+                in_=x_grouped[unit][:, first:end, :].rearrange("p n t -> p (n t)"),
+            )
+
+        def open_x_codes(unit):
             x_codes[unit] = keep.tile([P, NODES], U32, align_bytes=64, name="x_codes_%d" % unit)
             x_scales[unit] = keep.tile([P, NODES], U8, align_bytes=64, name="x_scales_%d" % unit)
-            nc.vector.quantize_mx(
-                out=x_codes[unit][:].bitcast(FP8X4),
-                scales=x_scales[unit][:],
-                in_=x_grouped[unit][:].rearrange("p n t -> p (n t)"),
-            )
 
         z_banks = {}
         stats = {}
         mean_var = {}
+        minus_mean_gain = {}
         rstd = {}
         y_scale = {}
         y_shift = {}
         y = {}
         negative_part = {}
 
-        def convolve(ot, b):
+        def convolve(ot, b, first=0, end=NODES):
             channels = slice(ot * P, (ot + 1) * P)
             if b == 0:
-                stats[ot] = small.tile([P, GRAPHS, BN_STATS_DIM], F32, name="stats_%d" % ot, tag="stats")
+                stats[ot] = small.tile([P, GRAPHS + (ot == 0), BN_STATS_DIM], F32, name="stats_%d" % ot, tag="stats")
             pool, tag = (early, "early_bank") if ot % 2 == 0 and b < 2 else (psum, "bank")
-            z_banks[ot, b] = pool.tile([P, NODES], F32, name="z_%d_%d" % (ot, b), tag=tag)
+            if first == 0:
+                z_banks[ot, b] = pool.tile([P, NODES], F32, name="z_%d_%d" % (ot, b), tag=tag)
             for g in range(K_GROUPS):
                 nc.tensor.matmul_mx(
-                    out=z_banks[ot, b][:],
+                    out=z_banks[ot, b][:, first:end],
                     lhsT=w_words[:, g, channels].bitcast(FP8X4),
                     lhsT_scale=w_scales[:, g, channels],
-                    rhs=x_codes[2 * b + g][:].bitcast(FP8X4),
-                    rhs_scale=x_scales[2 * b + g][:],
+                    rhs=x_codes[2 * b + g][:, first:end].bitcast(FP8X4),
+                    rhs_scale=x_scales[2 * b + g][:, first:end],
                     start=(g == 0),
                     stop=(g == K_GROUPS - 1),
                 )
 
-        def take_statistics(ot, b):
-            nc.vector.bn_stats(out=stats[ot][:, b, :], in_=z_banks[ot, b][:])
+        def take_statistics(ot, b, first=0, end=NODES):
+            nc.vector.bn_stats(out=stats[ot][:, b + (first > 0), :], in_=z_banks[ot, b][:, first:end])
 
         def aggregate_statistics(ot):
             mean_var[ot] = small.tile([P, 2], F32, name="mean_var_%d" % ot, tag="mean_var")
             nc.vector.bn_aggr(out=mean_var[ot][:], in_=stats[ot][:].rearrange("p b s -> p (b s)"))
+            minus_mean_gain[ot] = small.tile([P, 1], F32, name="minus_mean_gain_%d" % ot, tag="minus_mean_gain")
+            nc.gpsimd.tensor_mul(out=minus_mean_gain[ot][:], in0=mean_var[ot][:, 0:1], in1=gain_pm[:, ot, 1:2])
 
         def invert_deviation(ot):
             rstd[ot] = small.tile([P, 1], F32, name="rstd_%d" % ot, tag="rstd")
             nc.scalar.activation(out=rstd[ot][:], in_=mean_var[ot][:, 1:2], func=ACT.Abs_reciprocal_sqrt, bias=eps_bn[:])
 
         def make_scale(ot):
-            y_scale[ot] = small.tile([P, 2], F32, name="y_scale_%d" % ot, tag="y_scale")
-            nc.scalar.activation(out=y_scale[ot][:], in_=gain_pm[:, ot, :], func=ACT.Copy, scale=rstd[ot][:])
+            y_scale[ot] = small.tile([P, 1], F32, name="y_scale_%d" % ot, tag="y_scale")
+            nc.scalar.activation(out=y_scale[ot][:], in_=gain_pm[:, ot, 0:1], func=ACT.Copy, scale=rstd[ot][:])
 
         def make_shift(ot):
             y_shift[ot] = small.tile([P, 1], F32, name="y_shift_%d" % ot, tag="y_shift")
             nc.scalar.activation(
                 out=y_shift[ot][:],
-                in_=mean_var[ot][:, 0:1],
+                in_=minus_mean_gain[ot][:],
                 func=ACT.Identity,
-                scale=y_scale[ot][:, 1:2],
+                scale=rstd[ot][:],
                 bias=shift[:, ot : ot + 1],
             )
 
@@ -343,7 +355,7 @@ def tile_yuyipointupdate_pa_kernel(
                 out=y[ot][:, b * NODES : (b + 1) * NODES],
                 in_=z_banks[ot, b][:],
                 func=ACT.Identity,
-                scale=y_scale[ot][:, 0:1],
+                scale=y_scale[ot][:],
                 bias=y_shift[ot][:],
             )
 
@@ -351,7 +363,7 @@ def tile_yuyipointupdate_pa_kernel(
             nc.vector.tensor_scalar(
                 out=y[ot][:, b * NODES : (b + 1) * NODES],
                 in0=z_banks[ot, b][:],
-                scalar1=y_scale[ot][:, 0:1],
+                scalar1=y_scale[ot][:],
                 scalar2=y_shift[ot][:],
                 op0=ALU.mult,
                 op1=ALU.add,
@@ -386,10 +398,10 @@ def tile_yuyipointupdate_pa_kernel(
         def finish_shared(ot):
             leaky_on_vector(ot, slice(0, FIRST_COLUMNS))
             aggregate_statistics(ot + 1)
-            invert_deviation(ot + 1)
             negate_part(ot, slice(SHARED_COLUMN, 3 * NODES))
-            make_scale(ot + 1)
+            invert_deviation(ot + 1)
             negate_part(ot, slice(3 * NODES, 3 * NODES + 2 * P))
+            make_scale(ot + 1)
             make_shift(ot + 1)
             negate_part(ot, slice(3 * NODES + 2 * P, GRAPHS * NODES))
             leaky_on_vector(ot, slice(FIRST_COLUMNS, SHARED_COLUMN))
@@ -417,13 +429,6 @@ def tile_yuyipointupdate_pa_kernel(
         mask_diagonal(1)
         sum_rows(1, 0, 3)
         clamp_sums(0)
-        gain_shift_ps = psum.tile([P, P], BF16, tag="bank")
-        nc.tensor.transpose(gain_shift_ps[:], gain_shift_rows[:], ident_bf16[:])
-        gain_pm = const.tile([P, CHANNEL_TILES, 2], F32)
-        nc.vector.tensor_copy(out=gain_pm[:, :, 0], in_=gain_shift_ps[:, 0:CHANNEL_TILES])
-        nc.vector.tensor_scalar_mul(out=gain_pm[:, :, 1], in0=gain_shift_ps[:, 0:CHANNEL_TILES], scalar1=-1.0)
-        shift = const.tile([P, CHANNEL_TILES], F32)
-        nc.vector.tensor_copy(out=shift[:], in_=gain_shift_ps[:, CHANNEL_TILES : 2 * CHANNEL_TILES])
         sum_rows_on_vector(1, 3, 4)
         invert_sums(0)
         scale_rows(0)
@@ -474,10 +479,18 @@ def tile_yuyipointupdate_pa_kernel(
                 convolve(0, 1)
             if exists(i - 1) and exists(i + 4):
                 quantise_x(i - 1)
+            if i == 1:
+                gain_shift_ps = early.tile([P, P], BF16, tag="early_bank")
+                nc.tensor.transpose(gain_shift_ps[:], gain_shift_rows[:], ident_bf16[:])
+            if i == 2:
+                nc.vector.tensor_copy(out=gain_pm[:, :, 0], in_=gain_shift_ps[:, 0:CHANNEL_TILES])
+                nc.vector.tensor_scalar_mul(out=gain_pm[:, :, 1], in0=gain_shift_ps[:, 0:CHANNEL_TILES], scalar1=-1.0)
+                nc.vector.tensor_copy(out=shift[:], in_=gain_shift_ps[:, CHANNEL_TILES : 2 * CHANNEL_TILES])
             if i % 2 == 0 and exists(i + 2):
                 regroup_points((i + 2) // 2)
 
         last = UNITS - 1
+        half = NODES // 2
         quantise_edges(last)
         take_statistics(0, 1)
         aggregate(last, NODE_TILES - 1)
@@ -485,10 +498,13 @@ def tile_yuyipointupdate_pa_kernel(
         quantise_x(last - 1)
         convolve(0, 2)
         copy_x_on_vector(last, 3)
+        quantise_x(last, 0, half)
+        convolve(0, 3, 0, half)
         take_statistics(0, 2)
-        quantise_x(last)
-        convolve(0, 3)
-        take_statistics(0, 3)
+        quantise_x(last, half, NODES)
+        convolve(0, 3, half, NODES)
+        take_statistics(0, 3, 0, half)
+        take_statistics(0, 3, half, NODES)
         aggregate_statistics(0)
         invert_deviation(0)
         make_scale(0)

@@ -29,7 +29,7 @@ SIGN_CLEARED = 0x7FFF7FFF
 HEAD_UNITS = 3
 FOLD = 64
 FIRST_COLUMNS = 256
-SHARED_COLUMN = 1216
+SHARED_COLUMN = 1280
 SCALAR_ROW_TILES = 1
 
 FLOPS = 2 * GRAPHS * (2 * NODES * NODES * FEATURES + CHANNELS * CHANNELS * NODES)
@@ -204,7 +204,7 @@ def tile_yuyipointupdate_pa_kernel(
             )
 
         def clamp_sums(unit):
-            nc.gpsimd.tensor_scalar_max(out=row_sum[unit][:], in0=row_sum[unit][:], scalar1=EPS_L1)
+            nc.vector.tensor_scalar_max(out=row_sum[unit][:], in0=row_sum[unit][:], scalar1=EPS_L1)
 
         def invert_sums(unit):
             row_scale[unit] = small.tile([P, NODE_TILES], F32, name="row_scale_%d" % unit, tag="row_scale")
@@ -327,12 +327,14 @@ def tile_yuyipointupdate_pa_kernel(
         def aggregate_statistics(ot):
             mean_var[ot] = small.tile([P, 2], F32, name="mean_var_%d" % ot, tag="mean_var")
             nc.vector.bn_aggr(out=mean_var[ot][:], in_=stats[ot][:].rearrange("p b s -> p (b s)"))
-            minus_mean_gain[ot] = small.tile([P, 1], F32, name="minus_mean_gain_%d" % ot, tag="minus_mean_gain")
-            nc.gpsimd.tensor_mul(out=minus_mean_gain[ot][:], in0=mean_var[ot][:, 0:1], in1=gain_pm[:, ot, 1:2])
 
         def invert_deviation(ot):
             rstd[ot] = small.tile([P, 1], F32, name="rstd_%d" % ot, tag="rstd")
             nc.scalar.activation(out=rstd[ot][:], in_=mean_var[ot][:, 1:2], func=ACT.Abs_reciprocal_sqrt, bias=eps_bn[:])
+            minus_mean_gain[ot] = small.tile([P, 1], F32, name="minus_mean_gain_%d" % ot, tag="minus_mean_gain")
+            nc.scalar.activation(
+                out=minus_mean_gain[ot][:], in_=mean_var[ot][:, 0:1], func=ACT.Copy, scale=gain_pm[:, ot, 1:2]
+            )
 
         def make_scale(ot):
             y_scale[ot] = small.tile([P, 1], F32, name="y_scale_%d" % ot, tag="y_scale")

@@ -436,44 +436,50 @@ def tile_yuyipointupdate_pa_kernel(
         scale_rows(0)
         transpose_edges(0)
         regroup_points(0)
+        collect_transposed(0, 0)
+        collect_transposed(0, 1)
         mask_diagonal(2)
+        sum_rows(2)
         clamp_sums(1)
         quantise_points(0)
+        quantise_edges(0)
+        aggregate(0)
         invert_sums(1)
         mask_diagonal(3)
         scale_rows(1)
         transpose_edges(1)
-        collect_transposed(0, 0)
-        collect_transposed(0, 1)
-        sum_rows(2)
         take_magnitudes(3)
         fold_rows(3)
         for i in range(UNITS - 1):
-            quantise_edges(i)
-            if exists(i + 2):
-                clamp_sums(i + 2)
             if exists(i + 4):
                 mask_diagonal(i + 4)
+            if i > 0:
+                quantise_edges(i)
+            if exists(i + 2):
+                clamp_sums(i + 2)
+            if folds(i + 4):
+                take_magnitudes(i + 4)
             if i == UNITS - 2:
                 take_statistics(0, 0)
             if exists(i - 1) and not exists(i + 4):
                 quantise_x(i - 1)
             if exists(i + 2):
                 invert_sums(i + 2)
-            if folds(i + 3):
+            if i > 0 and folds(i + 3):
                 reduce_folded(i + 3)
+            if folds(i + 3):
                 sum_rows(i + 3, 0, SCALAR_ROW_TILES)
             if exists(i + 1):
                 collect_transposed(i + 1, 0)
                 collect_transposed(i + 1, 1)
-            aggregate(i, NODE_TILES - (1 if i == UNITS - 2 else 0))
+            if i > 0:
+                aggregate(i, NODE_TILES - (1 if i == UNITS - 2 else 0))
             if i % 2 == 1:
                 quantise_points((i + 1) // 2)
             if exists(i + 2):
                 scale_rows(i + 2)
                 transpose_edges(i + 2)
             if folds(i + 4):
-                take_magnitudes(i + 4)
                 fold_rows(i + 4)
             if i == 4:
                 convolve(0, 0)
@@ -490,6 +496,8 @@ def tile_yuyipointupdate_pa_kernel(
                 nc.vector.tensor_copy(out=shift[:], in_=gain_shift_ps[:, CHANNEL_TILES : 2 * CHANNEL_TILES])
             if i % 2 == 0 and exists(i + 2):
                 regroup_points((i + 2) // 2)
+            if i == 0:
+                reduce_folded(3)
 
         last = UNITS - 1
         half = NODES // 2

@@ -29,7 +29,7 @@ SIGN_CLEARED = 0x7FFF7FFF
 HEAD_UNITS = 3
 FOLD = 64
 FIRST_COLUMNS = 256
-SHARED_COLUMN = 1280
+SHARED_COLUMN = 1152
 SCALAR_ROW_TILES = 1
 
 FLOPS = 2 * GRAPHS * (2 * NODES * NODES * FEATURES + CHANNELS * CHANNELS * NODES)
@@ -114,6 +114,7 @@ def tile_yuyipointupdate_pa_kernel(
         point_grouped = {}
         row_sum = {}
         row_scale = {}
+        sums = {}
         magnitude = {}
         folded = {}
         transposed = {}
@@ -143,7 +144,10 @@ def tile_yuyipointupdate_pa_kernel(
 
         def mask_diagonal(unit, first=0, end=NODE_TILES):
             if first == 0:
-                row_sum[unit] = small.tile([P, NODE_TILES], F32, name="row_sum_%d" % unit, tag="row_sum")
+                paired = unit >= HEAD_UNITS and unit % 2 == 0
+                if not paired:
+                    sums[unit] = small.tile([P, 2 * NODE_TILES], F32, name="row_sum_%d" % unit, tag="row_sum")
+                row_sum[unit] = sums[unit - 1][:, NODE_TILES:] if paired else sums[unit][:, 0:NODE_TILES]
             diagonal_blocks = edge_sb[unit][:].rearrange("p r (c j) -> p (r c) j", j=P)[
                 :, first * (NODE_TILES + 1) : (end - 1) * (NODE_TILES + 1) + 1 : NODE_TILES + 1, :
             ]
@@ -203,12 +207,15 @@ def tile_yuyipointupdate_pa_kernel(
                 op=ALU.add,
             )
 
-        def clamp_sums(unit):
-            nc.vector.tensor_scalar_max(out=row_sum[unit][:], in0=row_sum[unit][:], scalar1=EPS_L1)
+        def clamp_sums(unit, count=1):
+            part = sums[unit][:, 0 : count * NODE_TILES]
+            nc.vector.tensor_scalar_max(out=part, in0=part, scalar1=EPS_L1)
 
-        def invert_sums(unit):
-            row_scale[unit] = small.tile([P, NODE_TILES], F32, name="row_scale_%d" % unit, tag="row_scale")
-            nc.vector.reciprocal(out=row_scale[unit][:], in_=row_sum[unit][:])
+        def invert_sums(unit, count=1):
+            scales = small.tile([P, 2 * NODE_TILES], F32, name="row_scale_%d" % unit, tag="row_scale")
+            nc.vector.reciprocal(out=scales[:, 0 : count * NODE_TILES], in_=sums[unit][:, 0 : count * NODE_TILES])
+            for k in range(count):
+                row_scale[unit + k] = scales[:, k * NODE_TILES : (k + 1) * NODE_TILES]
 
         def scale_rows(unit):
             for r in range(NODE_TILES):
@@ -429,9 +436,8 @@ def tile_yuyipointupdate_pa_kernel(
         sum_rows(0, 2, 3)
         sum_rows_on_vector(0, 3, 4)
         mask_diagonal(1)
-        sum_rows(1, 0, 3)
+        sum_rows(1, 0, 4)
         clamp_sums(0)
-        sum_rows_on_vector(1, 3, 4)
         invert_sums(0)
         scale_rows(0)
         transpose_edges(0)
@@ -450,25 +456,32 @@ def tile_yuyipointupdate_pa_kernel(
         transpose_edges(1)
         take_magnitudes(3)
         fold_rows(3)
+        sum_rows(3, 0, SCALAR_ROW_TILES)
         for i in range(UNITS - 1):
             if exists(i + 4):
                 mask_diagonal(i + 4)
+            if i % 2 == 1 and folds(i + 3):
+                reduce_folded(i + 3)
             if i > 0:
                 quantise_edges(i)
-            if exists(i + 2):
-                clamp_sums(i + 2)
+            if i == 0:
+                clamp_sums(2)
+            if i % 2 == 1:
+                clamp_sums(i + 2, 2 if exists(i + 3) else 1)
             if folds(i + 4):
                 take_magnitudes(i + 4)
             if i == UNITS - 2:
                 take_statistics(0, 0)
             if exists(i - 1) and not exists(i + 4):
                 quantise_x(i - 1)
-            if exists(i + 2):
-                invert_sums(i + 2)
-            if i > 0 and folds(i + 3):
+            if i == 0:
+                invert_sums(2)
+            if i % 2 == 1:
+                invert_sums(i + 2, 2 if exists(i + 3) else 1)
+            if i % 2 == 0 and i > 0 and folds(i + 3):
                 reduce_folded(i + 3)
-            if folds(i + 3):
-                sum_rows(i + 3, 0, SCALAR_ROW_TILES)
+            if folds(i + 4):
+                sum_rows(i + 4, 0, SCALAR_ROW_TILES)
             if exists(i + 1):
                 collect_transposed(i + 1, 0)
                 collect_transposed(i + 1, 1)
@@ -491,9 +504,9 @@ def tile_yuyipointupdate_pa_kernel(
                 gain_shift_ps = early.tile([P, P], BF16, tag="early_bank")
                 nc.tensor.transpose(gain_shift_ps[:], gain_shift_rows[:], ident_bf16[:])
             if i == 2:
-                nc.vector.tensor_copy(out=gain_pm[:, :, 0], in_=gain_shift_ps[:, 0:CHANNEL_TILES])
-                nc.vector.tensor_scalar_mul(out=gain_pm[:, :, 1], in0=gain_shift_ps[:, 0:CHANNEL_TILES], scalar1=-1.0)
-                nc.vector.tensor_copy(out=shift[:], in_=gain_shift_ps[:, CHANNEL_TILES : 2 * CHANNEL_TILES])
+                nc.scalar.copy(out=gain_pm[:, :, 0], in_=gain_shift_ps[:, 0:CHANNEL_TILES])
+                nc.scalar.mul(out=gain_pm[:, :, 1], in_=gain_shift_ps[:, 0:CHANNEL_TILES], mul=-1.0)
+                nc.scalar.copy(out=shift[:], in_=gain_shift_ps[:, CHANNEL_TILES : 2 * CHANNEL_TILES])
             if i % 2 == 0 and exists(i + 2):
                 regroup_points((i + 2) // 2)
             if i == 0:
@@ -503,11 +516,10 @@ def tile_yuyipointupdate_pa_kernel(
         half = NODES // 2
         quantise_edges(last)
         take_statistics(0, 1)
-        aggregate(last, NODE_TILES - 1)
+        aggregate(last, NODE_TILES - 0)
         copy_x_on_vector(last - 1, 3)
         quantise_x(last - 1)
         convolve(0, 2)
-        copy_x_on_vector(last, 3)
         quantise_x(last, 0, half)
         convolve(0, 3, 0, half)
         take_statistics(0, 2)

@@ -29,7 +29,7 @@ SIGN_CLEARED = 0x7FFF7FFF
 HEAD_UNITS = 3
 FOLD = 64
 FIRST_COLUMNS = 256
-SHARED_COLUMN = 1152
+SHARED_COLUMN = 1344
 SCALAR_ROW_TILES = 1
 
 FLOPS = 2 * GRAPHS * (2 * NODES * NODES * FEATURES + CHANNELS * CHANNELS * NODES)

@@ -29,7 +29,7 @@ SIGN_CLEARED = 0x7FFF7FFF
 HEAD_UNITS = 3
 FOLD = 64
 FIRST_COLUMNS = 256
-SHARED_COLUMN = 1344
+SHARED_COLUMN = 1280
 SCALAR_ROW_TILES = 1
 
 FLOPS = 2 * GRAPHS * (2 * NODES * NODES * FEATURES + CHANNELS * CHANNELS * NODES)
@@ -77,14 +77,14 @@ def tile_yuyipointupdate_pa_kernel(
         edge_sb = {}
         point_raw = {}
         def load_edges(unit):
-            edge_sb[unit] = inputs.tile([P, NODE_TILES, NODES], BF16, name="edge_%d" % unit)
+            edge_sb[unit] = inputs.tile([P, NODE_TILES, NODES], BF16, align_bytes=256, name="edge_%d" % unit)
             rows = edges[unit % 2][unit // 2].rearrange("(r p) m -> p r m", p=P)
             step = NODE_TILES // 2 if unit == 0 else NODE_TILES
             for r in range(0, NODE_TILES, step):
                 nc.sync.dma_start(out=edge_sb[unit][:, r : r + step, :], in_=rows[:, r : r + step, :])
 
         def load_points(b):
-            point_raw[b] = inputs.tile([P, PACK, FEATURES], BF16, name="point_%d" % b)
+            point_raw[b] = inputs.tile([P, PACK, FEATURES], BF16, align_bytes=256, name="point_%d" % b)
             nc.sync.dma_start(
                 out=point_raw[b][:].rearrange("q (u e) d -> q u e d", u=2),
                 in_=point_node[b].rearrange("(u q e) d -> q u e d", u=2, e=2),
@@ -100,7 +100,7 @@ def tile_yuyipointupdate_pa_kernel(
                     out=gain_shift_rows[CHANNEL_TILES : 2 * CHANNEL_TILES, :], in_=b1.rearrange("(t p) -> t p", p=P)
                 )
         load_points(GRAPHS - 1)
-        w_words = keep.tile([P, K_GROUPS, CHANNELS], U32, align_bytes=64)
+        w_words = keep.tile([P, K_GROUPS, CHANNELS], U32, align_bytes=256)
         for g in range(K_GROUPS):
             nc.sync.dma_start(
                 out=w_words[:, g, :].bitcast(I32), in_=W1_words[g].rearrange("p n t -> p (n t)").bitcast(I32)
@@ -359,7 +359,7 @@ def tile_yuyipointupdate_pa_kernel(
 
         def apply_affine(ot, b):
             if b == 0:
-                y[ot] = outputs.tile([P, GRAPHS * NODES], F32, name="y_%d" % ot, tag="y")
+                y[ot] = outputs.tile([P, GRAPHS * NODES], F32, align_bytes=256, name="y_%d" % ot, tag="y")
             nc.scalar.activation(
                 out=y[ot][:, b * NODES : (b + 1) * NODES],
                 in_=z_banks[ot, b][:],

@@ -29,7 +29,7 @@ SIGN_CLEARED = 0x7FFF7FFF
 HEAD_UNITS = 3
 FOLD = 64
 FIRST_COLUMNS = 256
-SHARED_COLUMN = 1280
+SHARED_COLUMN = 1216
 SCALAR_ROW_TILES = 1
 
 FLOPS = 2 * GRAPHS * (2 * NODES * NODES * FEATURES + CHANNELS * CHANNELS * NODES)
@@ -303,7 +303,6 @@ def tile_yuyipointupdate_pa_kernel(
         z_banks = {}
         stats = {}
         mean_var = {}
-        minus_mean_gain = {}
         rstd = {}
         y_scale = {}
         y_shift = {}
@@ -338,22 +337,18 @@ def tile_yuyipointupdate_pa_kernel(
         def invert_deviation(ot):
             rstd[ot] = small.tile([P, 1], F32, name="rstd_%d" % ot, tag="rstd")
             nc.scalar.activation(out=rstd[ot][:], in_=mean_var[ot][:, 1:2], func=ACT.Abs_reciprocal_sqrt, bias=eps_bn[:])
-            minus_mean_gain[ot] = small.tile([P, 1], F32, name="minus_mean_gain_%d" % ot, tag="minus_mean_gain")
-            nc.scalar.activation(
-                out=minus_mean_gain[ot][:], in_=mean_var[ot][:, 0:1], func=ACT.Copy, scale=gain_pm[:, ot, 1:2]
-            )
 
         def make_scale(ot):
-            y_scale[ot] = small.tile([P, 1], F32, name="y_scale_%d" % ot, tag="y_scale")
-            nc.scalar.activation(out=y_scale[ot][:], in_=gain_pm[:, ot, 0:1], func=ACT.Copy, scale=rstd[ot][:])
+            y_scale[ot] = small.tile([P, 2], F32, name="y_scale_%d" % ot, tag="y_scale")
+            nc.scalar.activation(out=y_scale[ot][:], in_=gain_pm[:, ot, :], func=ACT.Copy, scale=rstd[ot][:])
 
         def make_shift(ot):
             y_shift[ot] = small.tile([P, 1], F32, name="y_shift_%d" % ot, tag="y_shift")
             nc.scalar.activation(
                 out=y_shift[ot][:],
-                in_=minus_mean_gain[ot][:],
+                in_=mean_var[ot][:, 0:1],
                 func=ACT.Identity,
-                scale=rstd[ot][:],
+                scale=y_scale[ot][:, 1:2],
                 bias=shift[:, ot : ot + 1],
             )
 
@@ -364,7 +359,7 @@ def tile_yuyipointupdate_pa_kernel(
                 out=y[ot][:, b * NODES : (b + 1) * NODES],
                 in_=z_banks[ot, b][:],
                 func=ACT.Identity,
-                scale=y_scale[ot][:],
+                scale=y_scale[ot][:, 0:1],
                 bias=y_shift[ot][:],
             )
 
@@ -372,7 +367,7 @@ def tile_yuyipointupdate_pa_kernel(
             nc.vector.tensor_scalar(
                 out=y[ot][:, b * NODES : (b + 1) * NODES],
                 in0=z_banks[ot, b][:],
-                scalar1=y_scale[ot][:],
+                scalar1=y_scale[ot][:, 0:1],
                 scalar2=y_shift[ot][:],
                 op0=ALU.mult,
                 op1=ALU.add,
@@ -411,12 +406,14 @@ def tile_yuyipointupdate_pa_kernel(
             invert_deviation(ot + 1)
             negate_part(ot, slice(3 * NODES, 3 * NODES + 2 * P))
             make_scale(ot + 1)
-            make_shift(ot + 1)
             negate_part(ot, slice(3 * NODES + 2 * P, GRAPHS * NODES))
+            make_shift(ot + 1)
             leaky_on_vector(ot, slice(FIRST_COLUMNS, SHARED_COLUMN))
             store(ot, 0, 2)
-            leaky_on_gpsimd(ot, slice(SHARED_COLUMN, GRAPHS * NODES))
-            store(ot, 2, GRAPHS)
+            leaky_on_gpsimd(ot, slice(SHARED_COLUMN, 3 * NODES))
+            store(ot, 2, 3)
+            leaky_on_gpsimd(ot, slice(3 * NODES, GRAPHS * NODES))
+            store(ot, 3, GRAPHS)
 
         def finish_alone(ot):
             for b in range(GRAPHS):

from contextlib import ExitStack

import concourse.mybir as mybir
from concourse.masks import make_identity

F32 = mybir.dt.float32
BF16 = mybir.dt.bfloat16
I32 = mybir.dt.int32
U32 = mybir.dt.uint32
U8 = mybir.dt.uint8
FP8X4 = mybir.dt.float8_e4m3fn_x4
ALU = mybir.AluOpType
ACT = mybir.ActivationFunctionType

P = 128
PACK = 4
GRAPHS = 4
NODES = 512
FEATURES = 512
CHANNELS = 2 * FEATURES
NODE_TILES = NODES // P
CHANNEL_TILES = CHANNELS // P
K_GROUPS = CHANNELS // (P * PACK)
EPS_L1 = 1e-12
EPS_BN = 1e-5
NEG_SLOPE = 0.01
BN_STATS_DIM = 6
SIGN_CLEARED = 0x7FFF7FFF
HEAD_UNITS = 3
FOLD = 64
FIRST_COLUMNS = 256
SHARED_COLUMN = 1216
SCALAR_ROW_TILES = 1

FLOPS = 2 * GRAPHS * (2 * NODES * NODES * FEATURES + CHANNELS * CHANNELS * NODES)


UNITS = 2 * GRAPHS


def tile_yuyipointupdate_pa_kernel(
    tc, distribution_edge, instance_edge, point_node, W1_words, W1_scales, g1, b1, out
):
    nc = tc.nc
    edges = (distribution_edge, instance_edge)

    with ExitStack() as ctx:
        const = ctx.enter_context(tc.tile_pool(name="const", bufs=1))
        inputs = ctx.enter_context(tc.tile_pool(name="inputs", bufs=1))
        keep = ctx.enter_context(tc.tile_pool(name="keep", bufs=1))
        work = ctx.enter_context(tc.tile_pool(name="work", bufs=3))
        outputs = ctx.enter_context(tc.tile_pool(name="outputs", bufs=4))
        small = ctx.enter_context(tc.tile_pool(name="small", bufs=4))
        psum = ctx.enter_context(tc.psum_pool(name="psum", bufs=6))
        early = ctx.enter_context(tc.psum_pool(name="early", bufs=2))
        ctx.enter_context(tc.manual_schedule())

        eps_bn = const.tile([P, 1], F32)
        nc.vector.memset(eps_bn[:], EPS_BN)
        gain_shift_rows = const.tile([P, P], BF16)
        nc.vector.memset(gain_shift_rows[:], 0.0)
        gain_pm = const.tile([P, CHANNEL_TILES, 2], F32)
        shift = const.tile([P, CHANNEL_TILES], F32)
        table_loader = const.tile([P, 1], F32)
        nc.scalar.activation(out=table_loader[:], in_=eps_bn[:], func=ACT.Abs_reciprocal_sqrt)
        ident_f32 = const.tile([P, P], F32)
        make_identity(nc, ident_f32[:])
        ident_bf16 = const.tile([P, P], BF16)
        make_identity(nc, ident_bf16[:])
        off_diagonal = const.tile([P, P], BF16)
        nc.vector.tensor_scalar(
            out=off_diagonal[:], in0=ident_bf16[:], scalar1=-1.0, scalar2=1.0, op0=ALU.mult, op1=ALU.add
        )
        w_scales = keep.tile([P, K_GROUPS, CHANNELS], U8, align_bytes=64)
        nc.vector.memset(w_scales[:].rearrange("p g n -> p (g n)").bitcast(I32), 0)

        edge_sb = {}
        point_raw = {}
        def load_edges(unit):
            edge_sb[unit] = inputs.tile([P, NODE_TILES, NODES], BF16, align_bytes=256, name="edge_%d" % unit)
            rows = edges[unit % 2][unit // 2].rearrange("(r p) m -> p r m", p=P)
            step = NODE_TILES // 2 if unit == 0 else NODE_TILES
            for r in range(0, NODE_TILES, step):
                nc.sync.dma_start(out=edge_sb[unit][:, r : r + step, :], in_=rows[:, r : r + step, :])

        def load_points(b):
            point_raw[b] = inputs.tile([P, PACK, FEATURES], BF16, align_bytes=256, name="point_%d" % b)
            nc.sync.dma_start(
                out=point_raw[b][:].rearrange("q (u e) d -> q u e d", u=2),
                in_=point_node[b].rearrange("(u q e) d -> q u e d", u=2, e=2),
            )

        for unit in range(UNITS):
            load_edges(unit)
            if unit == 1 or unit >= 4 and unit % 2 == 0:
                load_points(max(0, unit // 2 - 1))
            if unit == 3:
                nc.sync.dma_start(out=gain_shift_rows[0:CHANNEL_TILES, :], in_=g1.rearrange("(t p) -> t p", p=P))
                nc.sync.dma_start(
                    out=gain_shift_rows[CHANNEL_TILES : 2 * CHANNEL_TILES, :], in_=b1.rearrange("(t p) -> t p", p=P)
                )
        load_points(GRAPHS - 1)
        w_words = keep.tile([P, K_GROUPS, CHANNELS], U32, align_bytes=256)
        for g in range(K_GROUPS):
            nc.sync.dma_start(
                out=w_words[:, g, :].bitcast(I32), in_=W1_words[g].rearrange("p n t -> p (n t)").bitcast(I32)
            )
        for quadrant in range(4):
            nc.sync.dma_start(
                out=w_scales[32 * quadrant : 32 * quadrant + 4, :, :].bitcast(I32),
                in_=W1_scales[:, 4 * quadrant : 4 * quadrant + 4, :].rearrange("g r n -> r g n").bitcast(I32),
            )

        point_grouped = {}
        row_sum = {}
        row_scale = {}
        sums = {}
        magnitude = {}
        folded = {}
        transposed = {}
        edge_grouped = {}
        edge_codes = {}
        edge_scales = {}
        point_codes = {}
        point_scales = {}
        x_grouped = {}
        x_codes = {}
        x_scales = {}

        def regroup_points(b):
            point_grouped[b] = work.tile([P, PACK, P, PACK], BF16, align_bytes=64, name="point_grouped_%d" % b, tag="point_grouped")
            nc.vector.tensor_copy(
                out=point_grouped[b][:], in_=point_raw[b][:].rearrange("q t (pp tt) -> q tt pp t", tt=PACK)
            )

        def quantise_points(b):
            point_codes[b] = work.tile([P, FEATURES], U32, align_bytes=64, name="point_codes_%d" % b, tag="point_codes")
            point_scales[b] = work.tile([P, FEATURES], U8, align_bytes=64, name="point_scales_%d" % b, tag="point_scales")
            nc.vector.quantize_mx(
                out=point_codes[b][:].bitcast(FP8X4),
                scales=point_scales[b][:],
                in_=point_grouped[b][:].rearrange("q tt pp t -> q (tt pp t)"),
            )

        def mask_diagonal(unit, first=0, end=NODE_TILES):
            if first == 0:
                paired = unit >= HEAD_UNITS and unit % 2 == 0
                if not paired:
                    sums[unit] = small.tile([P, 2 * NODE_TILES], F32, name="row_sum_%d" % unit, tag="row_sum")
                row_sum[unit] = sums[unit - 1][:, NODE_TILES:] if paired else sums[unit][:, 0:NODE_TILES]
            diagonal_blocks = edge_sb[unit][:].rearrange("p r (c j) -> p (r c) j", j=P)[
                :, first * (NODE_TILES + 1) : (end - 1) * (NODE_TILES + 1) + 1 : NODE_TILES + 1, :
            ]
            nc.vector.tensor_tensor(
                out=diagonal_blocks,
                in0=diagonal_blocks,
                in1=off_diagonal[:].unsqueeze(1).to_broadcast([P, end - first, P]),
                op=ALU.mult,
            )

        def sum_rows(unit, first=0, end=NODE_TILES):
            for r in range(first, end):
                magnitudes = work.tile([P, NODES], BF16)
                nc.scalar.activation(
                    out=magnitudes[:],
                    in_=edge_sb[unit][:, r, :],
                    func=ACT.Abs,
                    accum_out=row_sum[unit][:, r : r + 1],
                )

        def sum_rows_on_vector(unit, first, end):
            nc.vector.tensor_reduce(
                out=row_sum[unit][:, first:end],
                in_=edge_sb[unit][:, first:end, :],
                axis=mybir.AxisListType.X,
                op=ALU.add,
                apply_absolute_value=True,
            )

        def take_magnitudes(unit):
            magnitude[unit] = work.tile([P, NODE_TILES, NODES], BF16, name="magnitude_%d" % unit, tag="magnitude")
            nc.vector.tensor_scalar(
                out=magnitude[unit][:, SCALAR_ROW_TILES:, :].bitcast(I32),
                in0=edge_sb[unit][:, SCALAR_ROW_TILES:, :].bitcast(I32),
                scalar1=SIGN_CLEARED,
                scalar2=None,
                op0=ALU.bitwise_and,
            )

        def fold_rows(unit):
            folded[unit] = psum.tile([P, NODE_TILES, FOLD], F32, name="folded_%d" % unit, tag="bank")
            for r in range(SCALAR_ROW_TILES, NODE_TILES):
                for c in range(0, NODES, FOLD):
                    nc.tensor.matmul(
                        folded[unit][:, r, :],
                        lhsT=ident_bf16[:],
                        rhs=magnitude[unit][:, r, c : c + FOLD],
                        start=(c == 0),
                        stop=(c + FOLD == NODES),
                    )

        def reduce_folded(unit):
            nc.vector.tensor_reduce(
                out=row_sum[unit][:, SCALAR_ROW_TILES:],
                in_=folded[unit][:, SCALAR_ROW_TILES:, :],
                axis=mybir.AxisListType.X,
                op=ALU.add,
            )

        def clamp_sums(unit, count=1):
            part = sums[unit][:, 0 : count * NODE_TILES]
            nc.vector.tensor_scalar_max(out=part, in0=part, scalar1=EPS_L1)

        def invert_sums(unit, count=1):
            scales = small.tile([P, 2 * NODE_TILES], F32, name="row_scale_%d" % unit, tag="row_scale")
            nc.vector.reciprocal(out=scales[:, 0 : count * NODE_TILES], in_=sums[unit][:, 0 : count * NODE_TILES])
            for k in range(count):
                row_scale[unit + k] = scales[:, k * NODE_TILES : (k + 1) * NODE_TILES]

        def scale_rows(unit):
            for r in range(NODE_TILES):
                nc.vector.tensor_scalar_mul(
                    out=edge_sb[unit][:, r, :], in0=edge_sb[unit][:, r, :], scalar1=row_scale[unit][:, r : r + 1]
                )

        def transpose_edges(unit):
            edge_words = edge_sb[unit][:].bitcast(F32)
            for half in range(2):
                transposed[unit, half] = psum.tile([P, 2, 2, P], F32, name="transposed_%d_%d" % (unit, half), tag="bank")
                for r in range(2):
                    for u in range(2):
                        nc.tensor.transpose(
                            transposed[unit, half][:, r, u, :],
                            edge_words[:, 2 * half + r, u * P : (u + 1) * P],
                            ident_f32[:],
                        )

        def collect_transposed(unit, half):
            if half == 0:
                edge_grouped[unit] = work.tile([P, NODES, PACK], BF16, align_bytes=64, name="edge_grouped_%d" % unit, tag="edge_grouped")
            grouped_words = edge_grouped[unit][:].bitcast(F32)
            nc.scalar.copy(
                out=grouped_words[:, half * 2 * P : (half + 1) * 2 * P, :].rearrange("q (r n) u -> q r n u", r=2),
                in_=transposed[unit, half][:].rearrange("q r u n -> q r n u"),
            )

        def quantise_edges(unit):
            edge_codes[unit] = work.tile([P, NODES], U32, align_bytes=64, name="edge_codes_%d" % unit, tag="edge_codes")
            edge_scales[unit] = work.tile([P, NODES], U8, align_bytes=64, name="edge_scales_%d" % unit, tag="edge_scales")
            nc.vector.quantize_mx(
                out=edge_codes[unit][:].bitcast(FP8X4),
                scales=edge_scales[unit][:],
                in_=edge_grouped[unit][:].rearrange("q n t -> q (n t)"),
            )

        x_banks = {}

        def take_x_banks(unit):
            x_grouped[unit] = work.tile([P, NODES, PACK], BF16, align_bytes=64, name="x_grouped_%d" % unit, tag="x_grouped")
            x_banks[unit] = [
                psum.tile([P, PACK, P], F32, name="aggregated_%d_%d" % (unit, j), tag="bank") for j in range(NODE_TILES)
            ]

        def aggregate(unit, scalar_tiles=NODE_TILES):
            b = unit // 2
            if unit not in x_banks:
                take_x_banks(unit)
            for j in range(NODE_TILES):
                nodes = slice(j * P, (j + 1) * P)
                aggregated = x_banks[unit][j]
                for tt in range(PACK):
                    columns = slice(tt * P, (tt + 1) * P)
                    nc.tensor.matmul_mx(
                        out=aggregated[:, tt, :],
                        lhsT=point_codes[b][:, columns].bitcast(FP8X4),
                        lhsT_scale=point_scales[b][:, columns],
                        rhs=edge_codes[unit][:, nodes].bitcast(FP8X4),
                        rhs_scale=edge_scales[unit][:, nodes],
                        start=True,
                        stop=True,
                    )
                if j < scalar_tiles:
                    nc.scalar.copy(out=x_grouped[unit][:, nodes, :], in_=aggregated[:].rearrange("p t n -> p n t"))

        def copy_x_on_vector(unit, j):
            nc.vector.tensor_copy(
                out=x_grouped[unit][:, j * P : (j + 1) * P, :], in_=x_banks[unit][j][:].rearrange("p t n -> p n t")
            )

        def quantise_x(unit, first=0, end=NODES):
            if first == 0:
                open_x_codes(unit)
            nc.vector.quantize_mx(
                out=x_codes[unit][:, first:end].bitcast(FP8X4),
                scales=x_scales[unit][:, first:end],
                in_=x_grouped[unit][:, first:end, :].rearrange("p n t -> p (n t)"),
            )

        def open_x_codes(unit):
            x_codes[unit] = keep.tile([P, NODES], U32, align_bytes=64, name="x_codes_%d" % unit)
            x_scales[unit] = keep.tile([P, NODES], U8, align_bytes=64, name="x_scales_%d" % unit)

        z_banks = {}
        stats = {}
        mean_var = {}
        rstd = {}
        y_scale = {}
        y_shift = {}
        y = {}
        negative_part = {}

        def convolve(ot, b, first=0, end=NODES):
            channels = slice(ot * P, (ot + 1) * P)
            if b == 0:
                stats[ot] = small.tile([P, GRAPHS + (ot == 0), BN_STATS_DIM], F32, name="stats_%d" % ot, tag="stats")
            pool, tag = (early, "early_bank") if ot % 2 == 0 and b < 2 else (psum, "bank")
            if first == 0:
                z_banks[ot, b] = pool.tile([P, NODES], F32, name="z_%d_%d" % (ot, b), tag=tag)
            for g in range(K_GROUPS):
                nc.tensor.matmul_mx(
                    out=z_banks[ot, b][:, first:end],
                    lhsT=w_words[:, g, channels].bitcast(FP8X4),
                    lhsT_scale=w_scales[:, g, channels],
                    rhs=x_codes[2 * b + g][:, first:end].bitcast(FP8X4),
                    rhs_scale=x_scales[2 * b + g][:, first:end],
                    start=(g == 0),
                    stop=(g == K_GROUPS - 1),
                )

        def take_statistics(ot, b, first=0, end=NODES):
            nc.vector.bn_stats(out=stats[ot][:, b + (first > 0), :], in_=z_banks[ot, b][:, first:end])

        def aggregate_statistics(ot):
            mean_var[ot] = small.tile([P, 2], F32, name="mean_var_%d" % ot, tag="mean_var")
            nc.vector.bn_aggr(out=mean_var[ot][:], in_=stats[ot][:].rearrange("p b s -> p (b s)"))

        def invert_deviation(ot):
            rstd[ot] = small.tile([P, 1], F32, name="rstd_%d" % ot, tag="rstd")
            nc.scalar.activation(out=rstd[ot][:], in_=mean_var[ot][:, 1:2], func=ACT.Abs_reciprocal_sqrt, bias=eps_bn[:])

        def make_scale(ot):
            y_scale[ot] = small.tile([P, 2], F32, name="y_scale_%d" % ot, tag="y_scale")
            nc.scalar.activation(out=y_scale[ot][:], in_=gain_pm[:, ot, :], func=ACT.Copy, scale=rstd[ot][:])

        def make_shift(ot):
            y_shift[ot] = small.tile([P, 1], F32, name="y_shift_%d" % ot, tag="y_shift")
            nc.scalar.activation(
                out=y_shift[ot][:],
                in_=mean_var[ot][:, 0:1],
                func=ACT.Identity,
                scale=y_scale[ot][:, 1:2],
                bias=shift[:, ot : ot + 1],
            )

        def apply_affine(ot, b):
            if b == 0:
                y[ot] = outputs.tile([P, GRAPHS * NODES], F32, align_bytes=256, name="y_%d" % ot, tag="y")
            nc.scalar.activation(
                out=y[ot][:, b * NODES : (b + 1) * NODES],
                in_=z_banks[ot, b][:],
                func=ACT.Identity,
                scale=y_scale[ot][:, 0:1],
                bias=y_shift[ot][:],
            )

        def apply_affine_on_vector(ot, b):
            nc.vector.tensor_scalar(
                out=y[ot][:, b * NODES : (b + 1) * NODES],
                in0=z_banks[ot, b][:],
                scalar1=y_scale[ot][:, 0:1],
                scalar2=y_shift[ot][:],
                op0=ALU.mult,
                op1=ALU.add,
            )

        def leaky_on_vector(ot, columns):
            part = y[ot][:, columns]
            nc.vector.scalar_tensor_tensor(
                out=part, in0=part, scalar=NEG_SLOPE, in1=part, op0=ALU.mult, op1=ALU.max
            )

        def negate_part(ot, columns):
            if ot not in negative_part:
                negative_part[ot] = outputs.tile([P, GRAPHS * NODES], F32, name="negative_part_%d" % ot, tag="negative_part")
            nc.scalar.activation(
                out=negative_part[ot][:, columns],
                in_=y[ot][:, columns],
                func=ACT.Relu,
                scale=NEG_SLOPE - 1.0,
            )

        def leaky_on_gpsimd(ot, columns):
            part = y[ot][:, columns]
            nc.gpsimd.tensor_add(out=part, in0=part, in1=negative_part[ot][:, columns])

        def store(ot, first, end):
            nc.sync.dma_start(
                out=out[first:end, ot * P : (ot + 1) * P, :].rearrange("b p n -> p b n"),
                in_=y[ot][:, first * NODES : end * NODES].rearrange("p (b n) -> p b n", n=NODES),
            )

        def finish_shared(ot):
            leaky_on_vector(ot, slice(0, FIRST_COLUMNS))
            aggregate_statistics(ot + 1)
            negate_part(ot, slice(SHARED_COLUMN, 3 * NODES))
            invert_deviation(ot + 1)
            negate_part(ot, slice(3 * NODES, 3 * NODES + 2 * P))
            make_scale(ot + 1)
            negate_part(ot, slice(3 * NODES + 2 * P, GRAPHS * NODES))
            make_shift(ot + 1)
            leaky_on_vector(ot, slice(FIRST_COLUMNS, SHARED_COLUMN))
            store(ot, 0, 2)
            leaky_on_gpsimd(ot, slice(SHARED_COLUMN, 3 * NODES))
            store(ot, 2, 3)
            leaky_on_gpsimd(ot, slice(3 * NODES, GRAPHS * NODES))
            store(ot, 3, GRAPHS)

        def finish_alone(ot):
            for b in range(GRAPHS):
                leaky_on_vector(ot, slice(b * NODES, (b + 1) * NODES))
                store(ot, b, b + 1)

        def exists(unit):
            return 0 <= unit < UNITS

        def folds(unit):
            return HEAD_UNITS <= unit < UNITS

        mask_diagonal(0, 0, 2)
        sum_rows(0, 0, 1)
        sum_rows_on_vector(0, 1, 2)
        mask_diagonal(0, 2, 4)
        sum_rows(0, 2, 3)
        sum_rows_on_vector(0, 3, 4)
        mask_diagonal(1)
        sum_rows(1, 0, 4)
        clamp_sums(0)
        invert_sums(0)
        scale_rows(0)
        transpose_edges(0)
        regroup_points(0)
        collect_transposed(0, 0)
        collect_transposed(0, 1)
        mask_diagonal(2)
        sum_rows(2)
        clamp_sums(1)
        quantise_points(0)
        quantise_edges(0)
        aggregate(0)
        invert_sums(1)
        mask_diagonal(3)
        scale_rows(1)
        transpose_edges(1)
        take_magnitudes(3)
        fold_rows(3)
        sum_rows(3, 0, SCALAR_ROW_TILES)
        for i in range(UNITS - 1):
            if exists(i + 4):
                mask_diagonal(i + 4)
            if i % 2 == 1 and folds(i + 3):
                reduce_folded(i + 3)
            if i > 0:
                quantise_edges(i)
            if i == 0:
                clamp_sums(2)
            if i % 2 == 1:
                clamp_sums(i + 2, 2 if exists(i + 3) else 1)
            if folds(i + 4):
                take_magnitudes(i + 4)
            if i == UNITS - 2:
                take_statistics(0, 0)
            if exists(i - 1) and not exists(i + 4):
                quantise_x(i - 1)
            if i == 0:
                invert_sums(2)
            if i % 2 == 1:
                invert_sums(i + 2, 2 if exists(i + 3) else 1)
            if i % 2 == 0 and i > 0 and folds(i + 3):
                reduce_folded(i + 3)
            if folds(i + 4):
                sum_rows(i + 4, 0, SCALAR_ROW_TILES)
            if exists(i + 1):
                collect_transposed(i + 1, 0)
                collect_transposed(i + 1, 1)
            if i > 0:
                aggregate(i, NODE_TILES - (1 if i == UNITS - 2 else 0))
            if i % 2 == 1:
                quantise_points((i + 1) // 2)
            if exists(i + 2):
                scale_rows(i + 2)
                transpose_edges(i + 2)
            if folds(i + 4):
                fold_rows(i + 4)
            if i == 4:
                convolve(0, 0)
            if i == 5:
                convolve(0, 1)
            if exists(i - 1) and exists(i + 4):
                quantise_x(i - 1)
            if i == 1:
                gain_shift_ps = early.tile([P, P], BF16, tag="early_bank")
                nc.tensor.transpose(gain_shift_ps[:], gain_shift_rows[:], ident_bf16[:])
            if i == 2:
                nc.scalar.copy(out=gain_pm[:, :, 0], in_=gain_shift_ps[:, 0:CHANNEL_TILES])
                nc.scalar.mul(out=gain_pm[:, :, 1], in_=gain_shift_ps[:, 0:CHANNEL_TILES], mul=-1.0)
                nc.scalar.copy(out=shift[:], in_=gain_shift_ps[:, CHANNEL_TILES : 2 * CHANNEL_TILES])
            if i % 2 == 0 and exists(i + 2):
                regroup_points((i + 2) // 2)
            if i == 0:
                reduce_folded(3)

        last = UNITS - 1
        half = NODES // 2
        quantise_edges(last)
        take_statistics(0, 1)
        aggregate(last, NODE_TILES - 0)
        copy_x_on_vector(last - 1, 3)
        quantise_x(last - 1)
        convolve(0, 2)
        quantise_x(last, 0, half)
        convolve(0, 3, 0, half)
        take_statistics(0, 2)
        quantise_x(last, half, NODES)
        convolve(0, 3, half, NODES)
        take_statistics(0, 3, 0, half)
        take_statistics(0, 3, half, NODES)
        aggregate_statistics(0)
        invert_deviation(0)
        make_scale(0)
        make_shift(0)

        for ot in range(CHANNEL_TILES):
            for b in range(GRAPHS):
                apply_affine(ot, b)
            if ot + 1 < CHANNEL_TILES:
                for b in range(GRAPHS):
                    convolve(ot + 1, b)
                    take_statistics(ot + 1, b)
            if ot + 2 < CHANNEL_TILES:
                finish_shared(ot)
            else:
                if ot + 1 < CHANNEL_TILES:
                    aggregate_statistics(ot + 1)
                    invert_deviation(ot + 1)
                    make_scale(ot + 1)
                    make_shift(ot + 1)
                finish_alone(ot)
